import numpy as np
import ml_dtypes


def mxq(x, axis, fmt="e4m3"):
    dtype, down = {"e4m3": (ml_dtypes.float8_e4m3fn, 7), "e5m2": (ml_dtypes.float8_e5m2, 14)}[fmt]
    v = np.moveaxis(np.asarray(x, np.float32).astype(ml_dtypes.bfloat16).astype(np.float64), axis, -1)
    blocks = v.reshape(v.shape[:-1] + (-1, 32))
    amax = np.abs(blocks).max(-1, keepdims=True)
    byte = np.maximum(np.where(amax > 0, np.frexp(amax)[1] - 1 + 127, 0) - down, 1)
    scale = np.exp2(byte - 127.0)
    codes = (blocks / scale).astype(np.float32).astype(dtype).astype(np.float64)
    return np.moveaxis((codes * scale).reshape(v.shape), -1, axis)


WIDE = False


def mx_kscale(k):
    if not WIDE:
        return np.ones(k)
    levels = np.array([10, -10, 5, -5, 0])
    a = np.random.permutation(np.resize(levels, k // 512 * 4)).reshape(k // 512, 4)
    idx = np.arange(k)
    return np.exp2(a[idx // 512, idx % 128 // 32])


BF16 = ml_dtypes.bfloat16


def bf(x):
    return np.asarray(x, np.float32).astype(BF16)


def f64(x):
    return np.asarray(x).astype(np.float64)


B, S, I, O, NB, G = 4, 1024, 1024, 128, 5, 1


def setup_inputs():
    s = mx_kscale(I)
    return {"x": bf(np.random.standard_normal((B, S, I)) * s),
            "basis_coeffs": bf(np.random.standard_normal((I, O // G, NB)) / np.sqrt(I)),
            "linear_w": bf(np.random.standard_normal((O, I)) / np.sqrt(I) / s),
            "pathway_balance": bf(0.5 + 0.1 * np.random.standard_normal(2))}


def reference(x, basis_coeffs, linear_w, pathway_balance):
    x = f64(x)
    pathway_balance = f64(pathway_balance)
    shape = x.shape[:-1]
    x_flat = x.reshape(-1, I)
    x_norm = np.tanh(x_flat)
    powers = np.arange(NB, dtype=np.float64)
    basis = x_norm[..., None] ** powers
    bq = mxq(basis, 1, "e4m3").transpose(2, 0, 1)
    cq = mxq(f64(basis_coeffs), 0, "e4m3").transpose(2, 0, 1)
    nonlinear_out = (bq @ cq).sum(0)
    if G > 1:
        nonlinear_out = np.tile(nonlinear_out, (1, G))
    linear_out = mxq(x_flat, 1, "e4m3") @ mxq(f64(linear_w), 1, "e4m3").T
    y = pathway_balance[0] * nonlinear_out + pathway_balance[1] * linear_out
    return y.reshape(*shape, O)

@@ -1,0 +1,220 @@
+from contextlib import ExitStack
+
+import concourse.mybir as mybir
+from concourse.masks import make_identity
+
+FP8X4 = mybir.dt.float8_e4m3fn_x4
+BF16 = mybir.dt.bfloat16
+F32 = mybir.dt.float32
+U32 = mybir.dt.uint32
+U8 = mybir.dt.uint8
+ACT = mybir.ActivationFunctionType
+ALU = mybir.AluOpType
+
+P = 128
+ROWS = 4096
+K = 1024
+OUT = 128
+POWERS = 5
+R = 2
+W = R * K
+W4 = W // 4
+NCH = ROWS // (P * R)
+FLOPS = 2 * ROWS * K * OUT * (POWERS + 1)
+
+V_COPIES = (0,)
+
+
+def tile_kolmogorovarnoldlinear_t_kernel(tc, x, basis_coeffs, linear_w, pathway_balance, out):
+    nc = tc.nc
+    xf = x.flatten_outer_dims()
+    of = out.flatten_outer_dims()
+    with ExitStack() as ctx:
+        ctx.enter_context(tc.manual_schedule())
+        const = ctx.enter_context(tc.tile_pool(name="const", bufs=1))
+        xpool = ctx.enter_context(tc.tile_pool(name="xpool", bufs=NCH))
+        gpool = ctx.enter_context(tc.tile_pool(name="gpool", bufs=3))
+        fpool = ctx.enter_context(tc.tile_pool(name="fpool", bufs=2))
+        bpool = ctx.enter_context(tc.tile_pool(name="bpool", bufs=2))
+        cpool = ctx.enter_context(tc.tile_pool(name="cpool", bufs=3))
+        ypool = ctx.enter_context(tc.tile_pool(name="ypool", bufs=3))
+        tpsum = ctx.enter_context(tc.psum_pool(name="tpsum", bufs=5))
+        opsum = ctx.enter_context(tc.psum_pool(name="opsum", bufs=3))
+
+        xs = {}
+        xts = {}
+        xgs = {}
+        fs = {}
+        bs = {}
+        cs = {}
+        sps = {}
+        os_ = {}
+        tmps = {}
+
+        def load(c):
+            xs[c] = xpool.tile([P, R, K], BF16, name="xs")
+            nc.sync.dma_start(
+                out=xs[c][:],
+                in_=xf[c * P * R : (c + 1) * P * R, :].rearrange("(p j) k -> p j k", j=R),
+            )
+
+        def transpose_words(src_words):
+            xt = tpsum.tile([P, 4, P], F32, name="xt")
+            for b in range(4):
+                nc.tensor.transpose(xt[:, b, :], src_words[:, b * P : (b + 1) * P], ident[:])
+            return xt
+
+        def copy_out(engine_is_vector, dst_words, xt):
+            dst = dst_words.rearrange("p (g r u) -> p g r u", g=2, r=P, u=2)
+            src = xt[:].rearrange("p (g u) r -> p g r u", g=2, u=2)
+            if engine_is_vector:
+                nc.vector.tensor_copy(out=dst, in_=src)
+            else:
+                nc.scalar.copy(out=dst, in_=src)
+
+        def tr(c):
+            words = xs[c][:].bitcast(F32)
+            xts[c] = [transpose_words(words[:, j, :]) for j in range(R)]
+
+        def a_copy(c):
+            xgs[c] = gpool.tile([P, W], BF16, name="xg", align_bytes=64)
+            words = xgs[c][:].bitcast(F32)
+            for j in range(R):
+                on_vector = c == 0 or (c in V_COPIES and j == 1)
+                copy_out(on_vector, words[:, j * 512 : (j + 1) * 512], xts[c][j])
+
+        def s_tanh(c):
+            fs[c] = fpool.tile([P, 2 * W], F32, name="f")
+            nc.scalar.activation(out=fs[c][:, 0:W], in_=xgs[c][:], func=ACT.Tanh)
+
+        def s_sq(c):
+            nc.scalar.activation(out=fs[c][:, W : 2 * W], in_=fs[c][:, 0:W], func=ACT.Square)
+
+        def s_t4(c):
+            bs[c] = bpool.tile([P, 4 * W], BF16, name="b", align_bytes=64)
+            nc.scalar.activation(out=bs[c][:, 3 * W : 4 * W], in_=fs[c][:, W : 2 * W], func=ACT.Square)
+
+        def v_conv(c):
+            nc.vector.tensor_copy(out=bs[c][:, 0 : 2 * W], in_=fs[c][:])
+
+        def v_t3(c):
+            nc.vector.tensor_tensor(
+                out=bs[c][:, 2 * W : 3 * W], in0=fs[c][:, W : 2 * W], in1=fs[c][:, 0:W], op=ALU.mult
+            )
+
+        def quant(codes, planes, lo, hi, src):
+            nc.vector.quantize_mx(out=codes[:, lo:hi].bitcast(FP8X4), scales=planes[:, lo:hi], in_=src)
+
+        def v_qx(c):
+            cs[c] = cpool.tile([P, 5 * W4], U32, name="codes", align_bytes=64)
+            sps[c] = cpool.tile([P, 5 * W4], U8, name="planes", align_bytes=64)
+            quant(cs[c], sps[c], 0, W4, xgs[c][:])
+
+        def v_q12(c):
+            quant(cs[c], sps[c], W4, 3 * W4, bs[c][:, 0 : 2 * W])
+
+        def v_q34(c):
+            quant(cs[c], sps[c], 3 * W4, 5 * W4, bs[c][:, 2 * W : 4 * W])
+
+        def mx_pass(dst, lw, ls, wi, g, start, stop):
+            off = wi * 256 + g * P
+            nc.tensor.matmul_mx(
+                out=dst,
+                lhsT=lw.bitcast(FP8X4),
+                lhsT_scale=ls,
+                rhs=wc[:, off : off + P].bitcast(FP8X4),
+                rhs_scale=wsp[:, off : off + P],
+                start=start,
+                stop=stop,
+            )
+
+        def mx(c):
+            o = opsum.tile([P, R, 2, OUT], F32, name="o")
+            os_[c] = o
+            for j in range(R):
+                for n in range(POWERS):
+                    for g in range(2):
+                        if n == 0:
+                            lw, ls = onec[:], onesp[:]
+                        else:
+                            off = n * W4 + (j * 2 + g) * P
+                            lw, ls = cs[c][:, off : off + P], sps[c][:, off : off + P]
+                        mx_pass(o[:, j, 0, :], lw, ls, n, g, n == 0 and g == 0, n == POWERS - 1 and g == 1)
+                for g in range(2):
+                    off = (j * 2 + g) * P
+                    mx_pass(o[:, j, 1, :], cs[c][:, off : off + P], sps[c][:, off : off + P], POWERS, g, g == 0, g == 1)
+
+        def s_epi(c):
+            tmps[c] = ypool.tile([P, R, OUT], F32, name="tmp")
+            nc.scalar.activation(out=tmps[c][:], in_=os_[c][:, :, 1, :], func=ACT.Copy, scale=pb[:, 1:2])
+
+        def v_epi(c):
+            y = ypool.tile([P, R, OUT], F32, name="y")
+            nc.vector.scalar_tensor_tensor(
+                out=y[:], in0=os_[c][:, :, 0, :], scalar=pb[:, 0:1], in1=tmps[c][:], op0=ALU.mult, op1=ALU.add
+            )
+            nc.sync.dma_start(
+                out=of[c * P * R : (c + 1) * P * R, :].rearrange("(p j) o -> p j o", j=R), in_=y[:]
+            )
+
+        load(0)
+        lw_raw = const.tile([P, K], BF16, name="lw_raw")
+        nc.sync.dma_start(out=lw_raw[:], in_=linear_w)
+        bc_raw = const.tile([P, 4 * 2 * OUT * POWERS], BF16, name="bc_raw")
+        nc.sync.dma_start(
+            out=bc_raw[:].rearrange("q (b e f) -> q b e f", b=4, e=2),
+            in_=basis_coeffs.rearrange("(b q e) o n -> q b e (o n)", b=4, q=P, e=2),
+        )
+        pbb = const.tile([P, 2], BF16, name="pbb")
+        nc.sync.dma_start(out=pbb[:], in_=pathway_balance.partition_broadcast(P))
+        for c in range(1, NCH):
+            load(c)
+
+        ident = const.tile([P, P], F32, name="ident")
+        make_identity(nc, ident[:])
+        ones_b = const.tile([P, 4 * P], BF16, name="ones_b", align_bytes=64)
+        nc.vector.memset(ones_b[:], 1.0)
+        onec = const.tile([P, P], U32, name="onec", align_bytes=64)
+        onesp = const.tile([P, P], U8, name="onesp", align_bytes=64)
+        wg = const.tile([P, 6 * K], BF16, name="wg", align_bytes=64)
+        wc = const.tile([P, 6 * 256], U32, name="wc", align_bytes=64)
+        wsp = const.tile([P, 6 * 256], U8, name="wsp", align_bytes=64)
+        pb = const.tile([P, 2], F32, name="pb")
+
+        tr(0)
+        lwt = transpose_words(lw_raw[:].bitcast(F32))
+        a_copy(0)
+        nc.vector.quantize_mx(out=onec[:].bitcast(FP8X4), scales=onesp[:], in_=ones_b[:])
+        copy_out(True, wg[:].bitcast(F32)[:, 5 * 512 : 6 * 512], lwt)
+        nc.vector.tensor_copy(out=pb[:], in_=pbb[:])
+        bc_view = bc_raw[:].rearrange("q (g t o n) -> q g t o n", g=2, t=4, o=OUT, n=POWERS)
+        for n in range(POWERS):
+            nc.vector.tensor_copy(
+                out=wg[:, n * K : (n + 1) * K].rearrange("q (g o t) -> q g o t", g=2, o=OUT, t=4),
+                in_=bc_view[:, :, :, :, n].rearrange("q g t o -> q g o t"),
+            )
+        quant(wc, wsp, 0, 1024, wg[:, 0:4096])
+        quant(wc, wsp, 1024, 1536, wg[:, 4096:6144])
+
+        for p in range(NCH + 2):
+            if 0 <= p - 2:
+                mx(p - 2)
+            if p + 1 < NCH:
+                tr(p + 1)
+            if p < NCH:
+                s_tanh(p)
+                s_sq(p)
+            if 0 <= p - 2:
+                s_epi(p - 2)
+            if p < NCH:
+                s_t4(p)
+            if 0 <= p - 1 < NCH:
+                v_conv(p - 1)
+                v_t3(p - 1)
+                v_qx(p - 1)
+                v_q12(p - 1)
+                v_q34(p - 1)
+            if 0 <= p - 2:
+                v_epi(p - 2)
+            if p + 1 < NCH:
+                a_copy(p + 1)

@@ -16,30 +16,34 @@ ROWS = 4096
 K = 1024
 OUT = 128
 POWERS = 5
-R = 2
-W = R * K
-W4 = W // 4
-NCH = ROWS // (P * R)
 FLOPS = 2 * ROWS * K * OUT * (POWERS + 1)
 
-V_COPIES = (0,)
+SIZES = (2, 2, 2, 2, 2, 2, 2, 2, 2, 2, 2, 2, 2, 2, 1, 1, 1, 1)
+NCH = len(SIZES)
+assert sum(SIZES) * P == ROWS
+V_COPIES = {4: (1,), 8: (1,)}
+V_SQUARES = ()
+V_FOURTHS = ()
+AHEAD = 5
 
 
 def tile_kolmogorovarnoldlinear_t_kernel(tc, x, basis_coeffs, linear_w, pathway_balance, out):
     nc = tc.nc
     xf = x.flatten_outer_dims()
     of = out.flatten_outer_dims()
+    row0 = [P * sum(SIZES[:c]) for c in range(NCH)]
     with ExitStack() as ctx:
         ctx.enter_context(tc.manual_schedule())
         const = ctx.enter_context(tc.tile_pool(name="const", bufs=1))
-        xpool = ctx.enter_context(tc.tile_pool(name="xpool", bufs=NCH))
+        xpool = ctx.enter_context(tc.tile_pool(name="xpool", bufs=6))
         gpool = ctx.enter_context(tc.tile_pool(name="gpool", bufs=3))
-        fpool = ctx.enter_context(tc.tile_pool(name="fpool", bufs=2))
-        bpool = ctx.enter_context(tc.tile_pool(name="bpool", bufs=2))
+        fpool = ctx.enter_context(tc.tile_pool(name="fpool", bufs=3))
+        bpool = ctx.enter_context(tc.tile_pool(name="bpool", bufs=3))
         cpool = ctx.enter_context(tc.tile_pool(name="cpool", bufs=3))
         ypool = ctx.enter_context(tc.tile_pool(name="ypool", bufs=3))
-        tpsum = ctx.enter_context(tc.psum_pool(name="tpsum", bufs=5))
-        opsum = ctx.enter_context(tc.psum_pool(name="opsum", bufs=3))
+        tpsum = ctx.enter_context(tc.psum_pool(name="tpsum", bufs=4))
+        npsum = ctx.enter_context(tc.psum_pool(name="npsum", bufs=2))
+        lpsum = ctx.enter_context(tc.psum_pool(name="lpsum", bufs=2))
 
         xs = {}
         xts = {}
@@ -48,14 +52,21 @@ def tile_kolmogorovarnoldlinear_t_kernel(tc, x, basis_coeffs, linear_w, pathway_
         bs = {}
         cs = {}
         sps = {}
-        os_ = {}
+        accn = {}
+        accl = {}
         tmps = {}
 
+        def live(c):
+            return 0 <= c < NCH
+
         def load(c):
-            xs[c] = xpool.tile([P, R, K], BF16, name="xs")
+            if not live(c):
+                return
+            r = SIZES[c]
+            xs[c] = xpool.tile([P, r, K], BF16, name="xs")
             nc.sync.dma_start(
                 out=xs[c][:],
-                in_=xf[c * P * R : (c + 1) * P * R, :].rearrange("(p j) k -> p j k", j=R),
+                in_=xf[row0[c] : row0[c] + P * r, :].rearrange("(p j) k -> p j k", j=r),
             )
 
         def transpose_words(src_words):
@@ -64,57 +75,70 @@ def tile_kolmogorovarnoldlinear_t_kernel(tc, x, basis_coeffs, linear_w, pathway_
                 nc.tensor.transpose(xt[:, b, :], src_words[:, b * P : (b + 1) * P], ident[:])
             return xt
 
-        def copy_out(engine_is_vector, dst_words, xt):
+        def copy_out(on_vector, dst_words, xt):
             dst = dst_words.rearrange("p (g r u) -> p g r u", g=2, r=P, u=2)
             src = xt[:].rearrange("p (g u) r -> p g r u", g=2, u=2)
-            if engine_is_vector:
+            if on_vector:
                 nc.vector.tensor_copy(out=dst, in_=src)
             else:
                 nc.scalar.copy(out=dst, in_=src)
 
         def tr(c):
+            if not live(c):
+                return
             words = xs[c][:].bitcast(F32)
-            xts[c] = [transpose_words(words[:, j, :]) for j in range(R)]
+            xts[c] = [transpose_words(words[:, j, :]) for j in range(SIZES[c])]
 
         def a_copy(c):
-            xgs[c] = gpool.tile([P, W], BF16, name="xg", align_bytes=64)
+            if not live(c):
+                return
+            xgs[c] = gpool.tile([P, SIZES[c] * K], BF16, name="xg", align_bytes=64)
             words = xgs[c][:].bitcast(F32)
-            for j in range(R):
-                on_vector = c == 0 or (c in V_COPIES and j == 1)
-                copy_out(on_vector, words[:, j * 512 : (j + 1) * 512], xts[c][j])
+            for j in range(SIZES[c]):
+                copy_out(j in V_COPIES.get(c, ()), words[:, j * 512 : (j + 1) * 512], xts[c][j])
+
+        def square(on_vector, dst, src):
+            if on_vector:
+                nc.vector.tensor_tensor(out=dst, in0=src, in1=src, op=ALU.mult)
+            else:
+                nc.scalar.activation(out=dst, in_=src, func=ACT.Square)
 
         def s_tanh(c):
-            fs[c] = fpool.tile([P, 2 * W], F32, name="f")
-            nc.scalar.activation(out=fs[c][:, 0:W], in_=xgs[c][:], func=ACT.Tanh)
+            if not live(c):
+                return
+            w = SIZES[c] * K
+            fs[c] = fpool.tile([P, 2 * w], F32, name="f")
+            nc.scalar.activation(out=fs[c][:, 0:w], in_=xgs[c][:], func=ACT.Tanh)
 
-        def s_sq(c):
-            nc.scalar.activation(out=fs[c][:, W : 2 * W], in_=fs[c][:, 0:W], func=ACT.Square)
+        def sq(c):
+            if not live(c):
+                return
+            w = SIZES[c] * K
+            square(c in V_SQUARES, fs[c][:, w : 2 * w], fs[c][:, 0:w])
 
-        def s_t4(c):
-            bs[c] = bpool.tile([P, 4 * W], BF16, name="b", align_bytes=64)
-            nc.scalar.activation(out=bs[c][:, 3 * W : 4 * W], in_=fs[c][:, W : 2 * W], func=ACT.Square)
-
-        def v_conv(c):
-            nc.vector.tensor_copy(out=bs[c][:, 0 : 2 * W], in_=fs[c][:])
-
-        def v_t3(c):
-            nc.vector.tensor_tensor(
-                out=bs[c][:, 2 * W : 3 * W], in0=fs[c][:, W : 2 * W], in1=fs[c][:, 0:W], op=ALU.mult
-            )
+        def t4(c):
+            if not live(c):
+                return
+            w = SIZES[c] * K
+            bs[c] = bpool.tile([P, 4 * w], BF16, name="b", align_bytes=64)
+            square(c in V_FOURTHS, bs[c][:, 3 * w : 4 * w], fs[c][:, w : 2 * w])
 
         def quant(codes, planes, lo, hi, src):
             nc.vector.quantize_mx(out=codes[:, lo:hi].bitcast(FP8X4), scales=planes[:, lo:hi], in_=src)
 
-        def v_qx(c):
-            cs[c] = cpool.tile([P, 5 * W4], U32, name="codes", align_bytes=64)
-            sps[c] = cpool.tile([P, 5 * W4], U8, name="planes", align_bytes=64)
-            quant(cs[c], sps[c], 0, W4, xgs[c][:])
-
-        def v_q12(c):
-            quant(cs[c], sps[c], W4, 3 * W4, bs[c][:, 0 : 2 * W])
-
-        def v_q34(c):
-            quant(cs[c], sps[c], 3 * W4, 5 * W4, bs[c][:, 2 * W : 4 * W])
+        def v_work(c):
+            if not live(c):
+                return
+            w = SIZES[c] * K
+            w4 = w // 4
+            f, b = fs[c], bs[c]
+            nc.vector.tensor_copy(out=b[:, 0 : 2 * w], in_=f[:])
+            nc.vector.tensor_tensor(out=b[:, 2 * w : 3 * w], in0=f[:, w : 2 * w], in1=f[:, 0:w], op=ALU.mult)
+            cs[c] = cpool.tile([P, 5 * w4], U32, name="codes", align_bytes=64)
+            sps[c] = cpool.tile([P, 5 * w4], U8, name="planes", align_bytes=64)
+            quant(cs[c], sps[c], 0, w4, xgs[c][:])
+            quant(cs[c], sps[c], w4, 3 * w4, b[:, 0 : 2 * w])
+            quant(cs[c], sps[c], 3 * w4, 5 * w4, b[:, 2 * w : 4 * w])
 
         def mx_pass(dst, lw, ls, wi, g, start, stop):
             off = wi * 256 + g * P
@@ -129,45 +153,56 @@ def tile_kolmogorovarnoldlinear_t_kernel(tc, x, basis_coeffs, linear_w, pathway_
             )
 
         def mx(c):
-            o = opsum.tile([P, R, 2, OUT], F32, name="o")
-            os_[c] = o
-            for j in range(R):
+            if not live(c):
+                return
+            w4 = SIZES[c] * K // 4
+            accl[c] = lpsum.tile([P, SIZES[c], OUT], F32, name="accl")
+            accn[c] = npsum.tile([P, SIZES[c], OUT], F32, name="accn")
+            for j in range(SIZES[c]):
+                for g in range(2):
+                    off = (j * 2 + g) * P
+                    mx_pass(accl[c][:, j, :], cs[c][:, off : off + P], sps[c][:, off : off + P], POWERS, g, g == 0, g == 1)
+            for j in range(SIZES[c]):
                 for n in range(POWERS):
                     for g in range(2):
                         if n == 0:
                             lw, ls = onec[:], onesp[:]
                         else:
-                            off = n * W4 + (j * 2 + g) * P
+                            off = n * w4 + (j * 2 + g) * P
                             lw, ls = cs[c][:, off : off + P], sps[c][:, off : off + P]
-                        mx_pass(o[:, j, 0, :], lw, ls, n, g, n == 0 and g == 0, n == POWERS - 1 and g == 1)
-                for g in range(2):
-                    off = (j * 2 + g) * P
-                    mx_pass(o[:, j, 1, :], cs[c][:, off : off + P], sps[c][:, off : off + P], POWERS, g, g == 0, g == 1)
+                        mx_pass(accn[c][:, j, :], lw, ls, n, g, n == 0 and g == 0, n == POWERS - 1 and g == 1)
 
         def s_epi(c):
-            tmps[c] = ypool.tile([P, R, OUT], F32, name="tmp")
-            nc.scalar.activation(out=tmps[c][:], in_=os_[c][:, :, 1, :], func=ACT.Copy, scale=pb[:, 1:2])
+            if not live(c):
+                return
+            tmps[c] = ypool.tile([P, SIZES[c], OUT], F32, name="tmp")
+            nc.scalar.activation(out=tmps[c][:], in_=accl[c][:], func=ACT.Copy, scale=pb[:, 1:2])
 
         def v_epi(c):
-            y = ypool.tile([P, R, OUT], F32, name="y")
+            if not live(c):
+                return
+            r = SIZES[c]
+            y = ypool.tile([P, r, OUT], F32, name="y")
             nc.vector.scalar_tensor_tensor(
-                out=y[:], in0=os_[c][:, :, 0, :], scalar=pb[:, 0:1], in1=tmps[c][:], op0=ALU.mult, op1=ALU.add
+                out=y[:], in0=accn[c][:], scalar=pb[:, 0:1], in1=tmps[c][:], op0=ALU.mult, op1=ALU.add
             )
             nc.sync.dma_start(
-                out=of[c * P * R : (c + 1) * P * R, :].rearrange("(p j) o -> p j o", j=R), in_=y[:]
+                out=of[row0[c] : row0[c] + P * r, :].rearrange("(p j) o -> p j o", j=r), in_=y[:]
             )
 
         load(0)
+        half = 2 * 2 * OUT * POWERS
+        bc_raw = const.tile([P, 2 * half], BF16, name="bc_raw")
+        for g in range(2):
+            nc.sync.dma_start(
+                out=bc_raw[:, g * half : (g + 1) * half].rearrange("q (u e f) -> q u e f", u=2, e=2),
+                in_=basis_coeffs[g * 512 : (g + 1) * 512].rearrange("(u q e) o n -> q u e (o n)", u=2, q=P, e=2),
+            )
         lw_raw = const.tile([P, K], BF16, name="lw_raw")
         nc.sync.dma_start(out=lw_raw[:], in_=linear_w)
-        bc_raw = const.tile([P, 4 * 2 * OUT * POWERS], BF16, name="bc_raw")
-        nc.sync.dma_start(
-            out=bc_raw[:].rearrange("q (b e f) -> q b e f", b=4, e=2),
-            in_=basis_coeffs.rearrange("(b q e) o n -> q b e (o n)", b=4, q=P, e=2),
-        )
         pbb = const.tile([P, 2], BF16, name="pbb")
         nc.sync.dma_start(out=pbb[:], in_=pathway_balance.partition_broadcast(P))
-        for c in range(1, NCH):
+        for c in range(1, AHEAD):
             load(c)
 
         ident = const.tile([P, P], F32, name="ident")
@@ -182,39 +217,32 @@ def tile_kolmogorovarnoldlinear_t_kernel(tc, x, basis_coeffs, linear_w, pathway_
         pb = const.tile([P, 2], F32, name="pb")
 
         tr(0)
-        lwt = transpose_words(lw_raw[:].bitcast(F32))
         a_copy(0)
+        s_tanh(0)
         nc.vector.quantize_mx(out=onec[:].bitcast(FP8X4), scales=onesp[:], in_=ones_b[:])
+        bc_view = bc_raw[:].rearrange("q (g t o n) -> q g t o n", g=2, t=4, o=OUT, n=POWERS)
+        for g in range(2):
+            for n in range(POWERS):
+                dst = wg[:, n * K + g * 512 : n * K + (g + 1) * 512].rearrange("q (o t) -> q o t", o=OUT, t=4)
+                src = bc_view[:, g, :, :, n].rearrange("q t o -> q o t")
+                nc.vector.tensor_copy(out=dst, in_=src)
+        lwt = transpose_words(lw_raw[:].bitcast(F32))
         copy_out(True, wg[:].bitcast(F32)[:, 5 * 512 : 6 * 512], lwt)
         nc.vector.tensor_copy(out=pb[:], in_=pbb[:])
-        bc_view = bc_raw[:].rearrange("q (g t o n) -> q g t o n", g=2, t=4, o=OUT, n=POWERS)
-        for n in range(POWERS):
-            nc.vector.tensor_copy(
-                out=wg[:, n * K : (n + 1) * K].rearrange("q (g o t) -> q g o t", g=2, o=OUT, t=4),
-                in_=bc_view[:, :, :, :, n].rearrange("q g t o -> q g o t"),
-            )
-        quant(wc, wsp, 0, 1024, wg[:, 0:4096])
-        quant(wc, wsp, 1024, 1536, wg[:, 4096:6144])
+        tr(1)
+        a_copy(1)
 
-        for p in range(NCH + 2):
-            if 0 <= p - 2:
-                mx(p - 2)
-            if p + 1 < NCH:
-                tr(p + 1)
-            if p < NCH:
-                s_tanh(p)
-                s_sq(p)
-            if 0 <= p - 2:
-                s_epi(p - 2)
-            if p < NCH:
-                s_t4(p)
-            if 0 <= p - 1 < NCH:
-                v_conv(p - 1)
-                v_t3(p - 1)
-                v_qx(p - 1)
-                v_q12(p - 1)
-                v_q34(p - 1)
-            if 0 <= p - 2:
-                v_epi(p - 2)
-            if p + 1 < NCH:
-                a_copy(p + 1)
+        for p in range(NCH + 1):
+            load(p + AHEAD)
+            tr(p + 2)
+            mx(p - 1)
+            sq(p)
+            s_tanh(p + 1)
+            t4(p)
+            a_copy(p + 2)
+            s_epi(p - 1)
+            if p == 0:
+                quant(wc, wsp, 0, 1024, wg[:, 0:4096])
+                quant(wc, wsp, 1024, 1536, wg[:, 4096:6144])
+            v_work(p)
+            v_epi(p - 1)

@@ -21,8 +21,10 @@ FLOPS = 2 * ROWS * K * OUT * (POWERS + 1)
 SIZES = (2, 2, 2, 2, 2, 2, 2, 2, 2, 2, 2, 2, 2, 2, 1, 1, 1, 1)
 NCH = len(SIZES)
 assert sum(SIZES) * P == ROWS
-V_COPIES = {4: (1,), 8: (1,)}
+V_COPIES = {0: (0, 1), 1: (0, 1), 4: (1,), 8: (1,)}
 V_SQUARES = ()
+S_ROUNDS = (17,)
+WEIGHTS_AT = 1
 V_FOURTHS = ()
 AHEAD = 5
 
@@ -122,6 +124,8 @@ def tile_kolmogorovarnoldlinear_t_kernel(tc, x, basis_coeffs, linear_w, pathway_
             w = SIZES[c] * K
             bs[c] = bpool.tile([P, 4 * w], BF16, name="b", align_bytes=64)
             square(c in V_FOURTHS, bs[c][:, 3 * w : 4 * w], fs[c][:, w : 2 * w])
+            if c in S_ROUNDS:
+                nc.scalar.activation(out=bs[c][:, 0 : 2 * w], in_=fs[c][:], func=ACT.Copy)
 
         def quant(codes, planes, lo, hi, src):
             nc.vector.quantize_mx(out=codes[:, lo:hi].bitcast(FP8X4), scales=planes[:, lo:hi], in_=src)
@@ -132,13 +136,18 @@ def tile_kolmogorovarnoldlinear_t_kernel(tc, x, basis_coeffs, linear_w, pathway_
             w = SIZES[c] * K
             w4 = w // 4
             f, b = fs[c], bs[c]
-            nc.vector.tensor_copy(out=b[:, 0 : 2 * w], in_=f[:])
+            if c not in S_ROUNDS:
+                nc.vector.tensor_copy(out=b[:, 0 : 2 * w], in_=f[:])
             nc.vector.tensor_tensor(out=b[:, 2 * w : 3 * w], in0=f[:, w : 2 * w], in1=f[:, 0:w], op=ALU.mult)
             cs[c] = cpool.tile([P, 5 * w4], U32, name="codes", align_bytes=64)
             sps[c] = cpool.tile([P, 5 * w4], U8, name="planes", align_bytes=64)
             quant(cs[c], sps[c], 0, w4, xgs[c][:])
-            quant(cs[c], sps[c], w4, 3 * w4, b[:, 0 : 2 * w])
-            quant(cs[c], sps[c], 3 * w4, 5 * w4, b[:, 2 * w : 4 * w])
+            if c in S_ROUNDS:
+                quant(cs[c], sps[c], 3 * w4, 5 * w4, b[:, 2 * w : 4 * w])
+                quant(cs[c], sps[c], w4, 3 * w4, b[:, 0 : 2 * w])
+            else:
+                quant(cs[c], sps[c], w4, 3 * w4, b[:, 0 : 2 * w])
+                quant(cs[c], sps[c], 3 * w4, 5 * w4, b[:, 2 * w : 4 * w])
 
         def mx_pass(dst, lw, ls, wi, g, start, stop):
             off = wi * 256 + g * P
@@ -162,15 +171,16 @@ def tile_kolmogorovarnoldlinear_t_kernel(tc, x, basis_coeffs, linear_w, pathway_
                 for g in range(2):
                     off = (j * 2 + g) * P
                     mx_pass(accl[c][:, j, :], cs[c][:, off : off + P], sps[c][:, off : off + P], POWERS, g, g == 0, g == 1)
+            order = (0, 3, 4, 1, 2) if c in S_ROUNDS else (0, 1, 2, 3, 4)
             for j in range(SIZES[c]):
-                for n in range(POWERS):
+                for n in order:
                     for g in range(2):
                         if n == 0:
                             lw, ls = onec[:], onesp[:]
                         else:
                             off = n * w4 + (j * 2 + g) * P
                             lw, ls = cs[c][:, off : off + P], sps[c][:, off : off + P]
-                        mx_pass(accn[c][:, j, :], lw, ls, n, g, n == 0 and g == 0, n == POWERS - 1 and g == 1)
+                        mx_pass(accn[c][:, j, :], lw, ls, n, g, n == order[0] and g == 0, n == order[-1] and g == 1)
 
         def s_epi(c):
             if not live(c):
@@ -225,24 +235,28 @@ def tile_kolmogorovarnoldlinear_t_kernel(tc, x, basis_coeffs, linear_w, pathway_
             for n in range(POWERS):
                 dst = wg[:, n * K + g * 512 : n * K + (g + 1) * 512].rearrange("q (o t) -> q o t", o=OUT, t=4)
                 src = bc_view[:, g, :, :, n].rearrange("q t o -> q o t")
-                nc.vector.tensor_copy(out=dst, in_=src)
+                nc.gpsimd.tensor_scalar(out=dst, in0=src, scalar1=1.0, scalar2=0.0, op0=ALU.mult, op1=ALU.add)
         lwt = transpose_words(lw_raw[:].bitcast(F32))
-        copy_out(True, wg[:].bitcast(F32)[:, 5 * 512 : 6 * 512], lwt)
-        nc.vector.tensor_copy(out=pb[:], in_=pbb[:])
         tr(1)
         a_copy(1)
+        copy_out(True, wg[:].bitcast(F32)[:, 5 * 512 : 6 * 512], lwt)
+        nc.vector.tensor_copy(out=pb[:], in_=pbb[:])
 
         for p in range(NCH + 1):
+            due = list(range(p)) if p == WEIGHTS_AT + 1 else [p - 1] if p > WEIGHTS_AT + 1 else []
             load(p + AHEAD)
             tr(p + 2)
-            mx(p - 1)
+            for c in due:
+                mx(c)
             sq(p)
             s_tanh(p + 1)
             t4(p)
             a_copy(p + 2)
-            s_epi(p - 1)
-            if p == 0:
+            for c in due:
+                s_epi(c)
+            if p == WEIGHTS_AT:
                 quant(wc, wsp, 0, 1024, wg[:, 0:4096])
                 quant(wc, wsp, 1024, 1536, wg[:, 4096:6144])
             v_work(p)
-            v_epi(p - 1)
+            for c in due:
+                v_epi(c)

@@ -21,10 +21,10 @@ FLOPS = 2 * ROWS * K * OUT * (POWERS + 1)
 SIZES = (2, 2, 2, 2, 2, 2, 2, 2, 2, 2, 2, 2, 2, 2, 1, 1, 1, 1)
 NCH = len(SIZES)
 assert sum(SIZES) * P == ROWS
-V_COPIES = {0: (0, 1), 1: (0, 1), 4: (1,), 8: (1,)}
+V_COPIES = {0: (0, 1), 1: (0, 1)}
 V_SQUARES = ()
 S_ROUNDS = (17,)
-WEIGHTS_AT = 1
+WEIGHTS_AT = 0
 V_FOURTHS = ()
 AHEAD = 5
 
@@ -235,11 +235,11 @@ def tile_kolmogorovarnoldlinear_t_kernel(tc, x, basis_coeffs, linear_w, pathway_
             for n in range(POWERS):
                 dst = wg[:, n * K + g * 512 : n * K + (g + 1) * 512].rearrange("q (o t) -> q o t", o=OUT, t=4)
                 src = bc_view[:, g, :, :, n].rearrange("q t o -> q o t")
-                nc.gpsimd.tensor_scalar(out=dst, in0=src, scalar1=1.0, scalar2=0.0, op0=ALU.mult, op1=ALU.add)
+                nc.vector.tensor_copy(out=dst, in_=src)
         lwt = transpose_words(lw_raw[:].bitcast(F32))
         tr(1)
         a_copy(1)
-        copy_out(True, wg[:].bitcast(F32)[:, 5 * 512 : 6 * 512], lwt)
+        copy_out(False, wg[:].bitcast(F32)[:, 5 * 512 : 6 * 512], lwt)
         nc.vector.tensor_copy(out=pb[:], in_=pbb[:])
 
         for p in range(NCH + 1):

@@ -18,12 +18,12 @@ OUT = 128
 POWERS = 5
 FLOPS = 2 * ROWS * K * OUT * (POWERS + 1)
 
-SIZES = (2, 2, 2, 2, 2, 2, 2, 2, 2, 2, 2, 2, 2, 2, 1, 1, 1, 1)
+SIZES = (1, 1, 2, 2, 2, 2, 2, 2, 2, 2, 2, 2, 2, 2, 2, 1, 1, 1, 1)
 NCH = len(SIZES)
 assert sum(SIZES) * P == ROWS
-V_COPIES = {0: (0, 1), 1: (0, 1)}
+V_COPIES = {0: (0,), 1: (0,)}
 V_SQUARES = ()
-S_ROUNDS = (17,)
+S_ROUNDS = (18,)
 WEIGHTS_AT = 0
 V_FOURTHS = ()
 AHEAD = 5
@@ -201,6 +201,7 @@ def tile_kolmogorovarnoldlinear_t_kernel(tc, x, basis_coeffs, linear_w, pathway_
             )
 
         load(0)
+        load(1)
         half = 2 * 2 * OUT * POWERS
         bc_raw = const.tile([P, 2 * half], BF16, name="bc_raw")
         for g in range(2):
@@ -212,7 +213,7 @@ def tile_kolmogorovarnoldlinear_t_kernel(tc, x, basis_coeffs, linear_w, pathway_
         nc.sync.dma_start(out=lw_raw[:], in_=linear_w)
         pbb = const.tile([P, 2], BF16, name="pbb")
         nc.sync.dma_start(out=pbb[:], in_=pathway_balance.partition_broadcast(P))
-        for c in range(1, AHEAD):
+        for c in range(2, AHEAD):
             load(c)
 
         ident = const.tile([P, P], F32, name="ident")
@@ -227,8 +228,10 @@ def tile_kolmogorovarnoldlinear_t_kernel(tc, x, basis_coeffs, linear_w, pathway_
         pb = const.tile([P, 2], F32, name="pb")
 
         tr(0)
+        tr(1)
         a_copy(0)
         s_tanh(0)
+        a_copy(1)
         nc.vector.quantize_mx(out=onec[:].bitcast(FP8X4), scales=onesp[:], in_=ones_b[:])
         bc_view = bc_raw[:].rearrange("q (g t o n) -> q g t o n", g=2, t=4, o=OUT, n=POWERS)
         for g in range(2):
@@ -237,9 +240,7 @@ def tile_kolmogorovarnoldlinear_t_kernel(tc, x, basis_coeffs, linear_w, pathway_
                 src = bc_view[:, g, :, :, n].rearrange("q t o -> q o t")
                 nc.vector.tensor_copy(out=dst, in_=src)
         lwt = transpose_words(lw_raw[:].bitcast(F32))
-        tr(1)
-        a_copy(1)
-        copy_out(False, wg[:].bitcast(F32)[:, 5 * 512 : 6 * 512], lwt)
+        copy_out(True, wg[:].bitcast(F32)[:, 5 * 512 : 6 * 512], lwt)
         nc.vector.tensor_copy(out=pb[:], in_=pbb[:])
 
         for p in range(NCH + 1):

@@ -21,7 +21,10 @@ FLOPS = 2 * ROWS * K * OUT * (POWERS + 1)
 SIZES = (1, 1, 2, 2, 2, 2, 2, 2, 2, 2, 2, 2, 2, 2, 2, 1, 1, 1, 1)
 NCH = len(SIZES)
 assert sum(SIZES) * P == ROWS
-V_COPIES = {0: (0,), 1: (0,)}
+V_COPIES = {c: (0,) for c in range(NCH) if c < 2 or (SIZES[c] == 2 and c % 2 == 0)}
+G_COLS = 640
+G_CHUNKS = tuple(c for c in range(NCH) if SIZES[c] == 2)
+E_CHUNKS = G_CHUNKS
 V_SQUARES = ()
 S_ROUNDS = (18,)
 WEIGHTS_AT = 0
@@ -43,9 +46,10 @@ def tile_kolmogorovarnoldlinear_t_kernel(tc, x, basis_coeffs, linear_w, pathway_
         bpool = ctx.enter_context(tc.tile_pool(name="bpool", bufs=3))
         cpool = ctx.enter_context(tc.tile_pool(name="cpool", bufs=3))
         ypool = ctx.enter_context(tc.tile_pool(name="ypool", bufs=3))
+        sqpool = ctx.enter_context(tc.tile_pool(name="sqpool", bufs=1))
         tpsum = ctx.enter_context(tc.psum_pool(name="tpsum", bufs=4))
-        npsum = ctx.enter_context(tc.psum_pool(name="npsum", bufs=2))
-        lpsum = ctx.enter_context(tc.psum_pool(name="lpsum", bufs=2))
+        epsum = ctx.enter_context(tc.psum_pool(name="epsum", bufs=2))
+        apsum = ctx.enter_context(tc.psum_pool(name="apsum", bufs=2))
 
         xs = {}
         xts = {}
@@ -54,6 +58,8 @@ def tile_kolmogorovarnoldlinear_t_kernel(tc, x, basis_coeffs, linear_w, pathway_
         bs = {}
         cs = {}
         sps = {}
+        sbs = {}
+        ets = {}
         accn = {}
         accl = {}
         tmps = {}
@@ -91,13 +97,24 @@ def tile_kolmogorovarnoldlinear_t_kernel(tc, x, basis_coeffs, linear_w, pathway_
             words = xs[c][:].bitcast(F32)
             xts[c] = [transpose_words(words[:, j, :]) for j in range(SIZES[c])]
 
-        def a_copy(c):
+        def v_copies(c):
             if not live(c):
                 return
-            xgs[c] = gpool.tile([P, SIZES[c] * K], BF16, name="xg", align_bytes=64)
+            if c not in xgs:
+                xgs[c] = gpool.tile([P, SIZES[c] * K], BF16, name="xg", align_bytes=64)
+            words = xgs[c][:].bitcast(F32)
+            for j in V_COPIES.get(c, ()):
+                copy_out(True, words[:, j * 512 : (j + 1) * 512], xts[c][j])
+
+        def s_copies(c):
+            if not live(c):
+                return
+            if c not in xgs:
+                xgs[c] = gpool.tile([P, SIZES[c] * K], BF16, name="xg", align_bytes=64)
             words = xgs[c][:].bitcast(F32)
             for j in range(SIZES[c]):
-                copy_out(j in V_COPIES.get(c, ()), words[:, j * 512 : (j + 1) * 512], xts[c][j])
+                if j not in V_COPIES.get(c, ()):
+                    copy_out(False, words[:, j * 512 : (j + 1) * 512], xts[c][j])
 
         def square(on_vector, dst, src):
             if on_vector:
@@ -122,10 +139,42 @@ def tile_kolmogorovarnoldlinear_t_kernel(tc, x, basis_coeffs, linear_w, pathway_
             if not live(c):
                 return
             w = SIZES[c] * K
-            bs[c] = bpool.tile([P, 4 * w], BF16, name="b", align_bytes=64)
-            square(c in V_FOURTHS, bs[c][:, 3 * w : 4 * w], fs[c][:, w : 2 * w])
+            bs[c] = bpool.tile([P, 3 * w], BF16, name="b", align_bytes=64)
+            square(c in V_FOURTHS, bs[c][:, 2 * w : 3 * w], fs[c][:, w : 2 * w])
             if c in S_ROUNDS:
-                nc.scalar.activation(out=bs[c][:, 0 : 2 * w], in_=fs[c][:], func=ACT.Copy)
+                sbs[c] = sqpool.tile([P, w], BF16, name="sb", align_bytes=64)
+                nc.scalar.activation(out=bs[c][:, 0:w], in_=fs[c][:, 0:w], func=ACT.Copy)
+                nc.scalar.activation(out=sbs[c][:], in_=fs[c][:, w : 2 * w], func=ACT.Copy)
+
+        def t_to_psum(c):
+            if not live(c) or c not in E_CHUNKS:
+                return
+            ets[c] = []
+            for j in range(SIZES[c]):
+                et = epsum.tile([P, 512], F32, name="et")
+                nc.tensor.matmul(out=et[:], lhsT=ident[:], rhs=fs[c][:, j * 512 : (j + 1) * 512], start=True, stop=True)
+                ets[c].append(et)
+
+        def g_round(c):
+            if not live(c) or c in S_ROUNDS:
+                return
+            w = SIZES[c] * K
+            sbs[c] = sqpool.tile([P, w], BF16, name="sb", align_bytes=64)
+            if c in G_CHUNKS:
+                n = SIZES[c] * G_COLS
+                nc.gpsimd.tensor_scalar(
+                    out=sbs[c][:, 0:n], in0=fs[c][:, w : w + n], scalar1=1.0, scalar2=0.0, op0=ALU.mult, op1=ALU.add
+                )
+
+        def v_window(c):
+            if not live(c) or c not in E_CHUNKS:
+                return
+            w = SIZES[c] * K
+            for j in range(SIZES[c]):
+                lo = j * 512
+                nc.vector.tensor_tensor(
+                    out=bs[c][:, w + lo : w + lo + 512], in0=fs[c][:, w + lo : w + lo + 512], in1=ets[c][j][:], op=ALU.mult
+                )
 
         def quant(codes, planes, lo, hi, src):
             nc.vector.quantize_mx(out=codes[:, lo:hi].bitcast(FP8X4), scales=planes[:, lo:hi], in_=src)
@@ -135,19 +184,23 @@ def tile_kolmogorovarnoldlinear_t_kernel(tc, x, basis_coeffs, linear_w, pathway_
                 return
             w = SIZES[c] * K
             w4 = w // 4
-            f, b = fs[c], bs[c]
+            f, b, sb = fs[c], bs[c], sbs[c]
+            done = 512 * SIZES[c] if c in E_CHUNKS else 0
             if c not in S_ROUNDS:
-                nc.vector.tensor_copy(out=b[:, 0 : 2 * w], in_=f[:])
-            nc.vector.tensor_tensor(out=b[:, 2 * w : 3 * w], in0=f[:, w : 2 * w], in1=f[:, 0:w], op=ALU.mult)
+                n = SIZES[c] * G_COLS if c in G_CHUNKS else 0
+                nc.vector.tensor_copy(out=b[:, 0:w], in_=f[:, 0:w])
+                nc.vector.tensor_copy(out=sb[:, n:w], in_=f[:, w + n : 2 * w])
+            nc.vector.tensor_tensor(out=b[:, w + done : 2 * w], in0=f[:, w + done : 2 * w], in1=f[:, done:w], op=ALU.mult)
             cs[c] = cpool.tile([P, 5 * w4], U32, name="codes", align_bytes=64)
             sps[c] = cpool.tile([P, 5 * w4], U8, name="planes", align_bytes=64)
             quant(cs[c], sps[c], 0, w4, xgs[c][:])
             if c in S_ROUNDS:
-                quant(cs[c], sps[c], 3 * w4, 5 * w4, b[:, 2 * w : 4 * w])
-                quant(cs[c], sps[c], w4, 3 * w4, b[:, 0 : 2 * w])
+                quant(cs[c], sps[c], 3 * w4, 5 * w4, b[:, w : 3 * w])
+                quant(cs[c], sps[c], w4, 2 * w4, b[:, 0:w])
             else:
-                quant(cs[c], sps[c], w4, 3 * w4, b[:, 0 : 2 * w])
-                quant(cs[c], sps[c], 3 * w4, 5 * w4, b[:, 2 * w : 4 * w])
+                quant(cs[c], sps[c], w4, 2 * w4, b[:, 0:w])
+                quant(cs[c], sps[c], 3 * w4, 5 * w4, b[:, w : 3 * w])
+            quant(cs[c], sps[c], 2 * w4, 3 * w4, sb[:])
 
         def mx_pass(dst, lw, ls, wi, g, start, stop):
             off = wi * 256 + g * P
@@ -165,8 +218,8 @@ def tile_kolmogorovarnoldlinear_t_kernel(tc, x, basis_coeffs, linear_w, pathway_
             if not live(c):
                 return
             w4 = SIZES[c] * K // 4
-            accl[c] = lpsum.tile([P, SIZES[c], OUT], F32, name="accl")
-            accn[c] = npsum.tile([P, SIZES[c], OUT], F32, name="accn")
+            acc = apsum.tile([P, 2, SIZES[c], OUT], F32, name="acc")
+            accl[c], accn[c] = acc[:, 0], acc[:, 1]
             for j in range(SIZES[c]):
                 for g in range(2):
                     off = (j * 2 + g) * P
@@ -186,7 +239,7 @@ def tile_kolmogorovarnoldlinear_t_kernel(tc, x, basis_coeffs, linear_w, pathway_
             if not live(c):
                 return
             tmps[c] = ypool.tile([P, SIZES[c], OUT], F32, name="tmp")
-            nc.scalar.activation(out=tmps[c][:], in_=accl[c][:], func=ACT.Copy, scale=pb[:, 1:2])
+            nc.scalar.activation(out=tmps[c][:], in_=accl[c], func=ACT.Copy, scale=pb[:, 1:2])
 
         def v_epi(c):
             if not live(c):
@@ -194,7 +247,7 @@ def tile_kolmogorovarnoldlinear_t_kernel(tc, x, basis_coeffs, linear_w, pathway_
             r = SIZES[c]
             y = ypool.tile([P, r, OUT], F32, name="y")
             nc.vector.scalar_tensor_tensor(
-                out=y[:], in0=accn[c][:], scalar=pb[:, 0:1], in1=tmps[c][:], op0=ALU.mult, op1=ALU.add
+                out=y[:], in0=accn[c], scalar=pb[:, 0:1], in1=tmps[c][:], op0=ALU.mult, op1=ALU.add
             )
             nc.sync.dma_start(
                 out=of[row0[c] : row0[c] + P * r, :].rearrange("(p j) o -> p j o", j=r), in_=y[:]
@@ -229,9 +282,9 @@ def tile_kolmogorovarnoldlinear_t_kernel(tc, x, basis_coeffs, linear_w, pathway_
 
         tr(0)
         tr(1)
-        a_copy(0)
+        v_copies(0)
         s_tanh(0)
-        a_copy(1)
+        v_copies(1)
         nc.vector.quantize_mx(out=onec[:].bitcast(FP8X4), scales=onesp[:], in_=ones_b[:])
         bc_view = bc_raw[:].rearrange("q (g t o n) -> q g t o n", g=2, t=4, o=OUT, n=POWERS)
         for g in range(2):
@@ -243,21 +296,27 @@ def tile_kolmogorovarnoldlinear_t_kernel(tc, x, basis_coeffs, linear_w, pathway_
         copy_out(True, wg[:].bitcast(F32)[:, 5 * 512 : 6 * 512], lwt)
         nc.vector.tensor_copy(out=pb[:], in_=pbb[:])
 
-        for p in range(NCH + 1):
+        for p in range(NCH + 2):
             due = list(range(p)) if p == WEIGHTS_AT + 1 else [p - 1] if p > WEIGHTS_AT + 1 else []
+            sums = [p - 2] if p >= 2 else []
             load(p + AHEAD)
+            t_to_psum(p)
             tr(p + 2)
             for c in due:
-                mx(c)
+                if live(c):
+                    mx(c)
             sq(p)
+            for c in sums:
+                s_epi(c)
             s_tanh(p + 1)
             t4(p)
-            a_copy(p + 2)
-            for c in due:
-                s_epi(c)
+            g_round(p)
+            s_copies(p + 2)
             if p == WEIGHTS_AT:
                 quant(wc, wsp, 0, 1024, wg[:, 0:4096])
                 quant(wc, wsp, 1024, 1536, wg[:, 4096:6144])
-            v_work(p)
-            for c in due:
+            v_window(p)
+            v_copies(p + 2)
+            for c in sums:
                 v_epi(c)
+            v_work(p)

@@ -22,7 +22,7 @@ SIZES = (1, 1, 2, 2, 2, 2, 2, 2, 2, 2, 2, 2, 2, 2, 2, 1, 1, 1, 1)
 NCH = len(SIZES)
 assert sum(SIZES) * P == ROWS
 V_COPIES = {c: (0,) for c in range(NCH) if c < 2 or (SIZES[c] == 2 and c % 2 == 0)}
-G_COLS = 640
+G_COLS = {c: 640 if c in V_COPIES else 416 for c in range(NCH)}
 G_CHUNKS = tuple(c for c in range(NCH) if SIZES[c] == 2)
 E_CHUNKS = G_CHUNKS
 V_SQUARES = ()
@@ -30,6 +30,7 @@ S_ROUNDS = (18,)
 WEIGHTS_AT = 0
 V_FOURTHS = ()
 AHEAD = 5
+PSUM_TANH = (0, 1)
 
 
 def tile_kolmogorovarnoldlinear_t_kernel(tc, x, basis_coeffs, linear_w, pathway_balance, out):
@@ -72,10 +73,11 @@ def tile_kolmogorovarnoldlinear_t_kernel(tc, x, basis_coeffs, linear_w, pathway_
                 return
             r = SIZES[c]
             xs[c] = xpool.tile([P, r, K], BF16, name="xs")
-            nc.sync.dma_start(
-                out=xs[c][:],
-                in_=xf[row0[c] : row0[c] + P * r, :].rearrange("(p j) k -> p j k", j=r),
-            )
+            src = xf[row0[c] : row0[c] + P * r, :].rearrange("(p j) k -> p j k", j=r)
+            parts = 2 if c == 0 else 1
+            for i in range(parts):
+                cols = slice(i * K // parts, (i + 1) * K // parts)
+                nc.sync.dma_start(out=xs[c][:, :, cols], in_=src[:, :, cols])
 
         def transpose_words(src_words):
             xt = tpsum.tile([P, 4, P], F32, name="xt")
@@ -97,11 +99,14 @@ def tile_kolmogorovarnoldlinear_t_kernel(tc, x, basis_coeffs, linear_w, pathway_
             words = xs[c][:].bitcast(F32)
             xts[c] = [transpose_words(words[:, j, :]) for j in range(SIZES[c])]
 
+        def new_xg(c):
+            if c not in xgs:
+                xgs[c] = gpool.tile([P, SIZES[c] * K], BF16, name="xg", align_bytes=64)
+
         def v_copies(c):
             if not live(c):
                 return
-            if c not in xgs:
-                xgs[c] = gpool.tile([P, SIZES[c] * K], BF16, name="xg", align_bytes=64)
+            new_xg(c)
             words = xgs[c][:].bitcast(F32)
             for j in V_COPIES.get(c, ()):
                 copy_out(True, words[:, j * 512 : (j + 1) * 512], xts[c][j])
@@ -109,8 +114,7 @@ def tile_kolmogorovarnoldlinear_t_kernel(tc, x, basis_coeffs, linear_w, pathway_
         def s_copies(c):
             if not live(c):
                 return
-            if c not in xgs:
-                xgs[c] = gpool.tile([P, SIZES[c] * K], BF16, name="xg", align_bytes=64)
+            new_xg(c)
             words = xgs[c][:].bitcast(F32)
             for j in range(SIZES[c]):
                 if j not in V_COPIES.get(c, ()):
@@ -127,7 +131,15 @@ def tile_kolmogorovarnoldlinear_t_kernel(tc, x, basis_coeffs, linear_w, pathway_
                 return
             w = SIZES[c] * K
             fs[c] = fpool.tile([P, 2 * w], F32, name="f")
-            nc.scalar.activation(out=fs[c][:, 0:w], in_=xgs[c][:], func=ACT.Tanh)
+            if c in PSUM_TANH:
+                for g in range(2):
+                    nc.scalar.activation(
+                        out=fs[c][:, g * 512 : (g + 1) * 512].rearrange("p (r u e) -> p r u e", r=P, u=2, e=2),
+                        in_=xts[c][0][:, 2 * g : 2 * g + 2, :].bitcast(BF16).rearrange("p u (r e) -> p r u e", r=P, e=2),
+                        func=ACT.Tanh,
+                    )
+            else:
+                nc.scalar.activation(out=fs[c][:, 0:w], in_=xgs[c][:], func=ACT.Tanh)
 
         def sq(c):
             if not live(c):
@@ -161,7 +173,7 @@ def tile_kolmogorovarnoldlinear_t_kernel(tc, x, basis_coeffs, linear_w, pathway_
             w = SIZES[c] * K
             sbs[c] = sqpool.tile([P, w], BF16, name="sb", align_bytes=64)
             if c in G_CHUNKS:
-                n = SIZES[c] * G_COLS
+                n = SIZES[c] * G_COLS[c]
                 nc.gpsimd.tensor_scalar(
                     out=sbs[c][:, 0:n], in0=fs[c][:, w : w + n], scalar1=1.0, scalar2=0.0, op0=ALU.mult, op1=ALU.add
                 )
@@ -187,7 +199,7 @@ def tile_kolmogorovarnoldlinear_t_kernel(tc, x, basis_coeffs, linear_w, pathway_
             f, b, sb = fs[c], bs[c], sbs[c]
             done = 512 * SIZES[c] if c in E_CHUNKS else 0
             if c not in S_ROUNDS:
-                n = SIZES[c] * G_COLS if c in G_CHUNKS else 0
+                n = SIZES[c] * G_COLS[c] if c in G_CHUNKS else 0
                 nc.vector.tensor_copy(out=b[:, 0:w], in_=f[:, 0:w])
                 nc.vector.tensor_copy(out=sb[:, n:w], in_=f[:, w + n : 2 * w])
             nc.vector.tensor_tensor(out=b[:, w + done : 2 * w], in0=f[:, w + done : 2 * w], in1=f[:, done:w], op=ALU.mult)
@@ -253,20 +265,25 @@ def tile_kolmogorovarnoldlinear_t_kernel(tc, x, basis_coeffs, linear_w, pathway_
                 out=of[row0[c] : row0[c] + P * r, :].rearrange("(p j) o -> p j o", j=r), in_=y[:]
             )
 
-        load(0)
-        load(1)
         half = 2 * 2 * OUT * POWERS
         bc_raw = const.tile([P, 2 * half], BF16, name="bc_raw")
-        for g in range(2):
+
+        def load_coeffs(g):
             nc.sync.dma_start(
                 out=bc_raw[:, g * half : (g + 1) * half].rearrange("q (u e f) -> q u e f", u=2, e=2),
                 in_=basis_coeffs[g * 512 : (g + 1) * 512].rearrange("(u q e) o n -> q u e (o n)", u=2, q=P, e=2),
             )
+
+        load(0)
+        load(1)
+        load_coeffs(0)
+        load(2)
+        load_coeffs(1)
         lw_raw = const.tile([P, K], BF16, name="lw_raw")
         nc.sync.dma_start(out=lw_raw[:], in_=linear_w)
         pbb = const.tile([P, 2], BF16, name="pbb")
         nc.sync.dma_start(out=pbb[:], in_=pathway_balance.partition_broadcast(P))
-        for c in range(2, AHEAD):
+        for c in range(3, AHEAD):
             load(c)
 
         ident = const.tile([P, P], F32, name="ident")
@@ -275,48 +292,63 @@ def tile_kolmogorovarnoldlinear_t_kernel(tc, x, basis_coeffs, linear_w, pathway_
         nc.vector.memset(ones_b[:], 1.0)
         onec = const.tile([P, P], U32, name="onec", align_bytes=64)
         onesp = const.tile([P, P], U8, name="onesp", align_bytes=64)
+        nc.vector.quantize_mx(out=onec[:].bitcast(FP8X4), scales=onesp[:], in_=ones_b[:])
         wg = const.tile([P, 6 * K], BF16, name="wg", align_bytes=64)
         wc = const.tile([P, 6 * 256], U32, name="wc", align_bytes=64)
         wsp = const.tile([P, 6 * 256], U8, name="wsp", align_bytes=64)
         pb = const.tile([P, 2], F32, name="pb")
+        bc_view = bc_raw[:].rearrange("q (g t o n) -> q g t o n", g=2, t=4, o=OUT, n=POWERS)
+        wg_view = wg[:, 0 : POWERS * K].rearrange("q (n g o t) -> q n g o t", n=POWERS, g=2, o=OUT, t=4)
+
+        def regroup(g):
+            for n in range(POWERS):
+                nc.vector.tensor_copy(out=wg_view[:, n, g], in_=bc_view[:, g, :, :, n].rearrange("q t o -> q o t"))
 
         tr(0)
         tr(1)
-        v_copies(0)
         s_tanh(0)
-        v_copies(1)
-        nc.vector.quantize_mx(out=onec[:].bitcast(FP8X4), scales=onesp[:], in_=ones_b[:])
-        bc_view = bc_raw[:].rearrange("q (g t o n) -> q g t o n", g=2, t=4, o=OUT, n=POWERS)
-        for g in range(2):
-            for n in range(POWERS):
-                dst = wg[:, n * K + g * 512 : n * K + (g + 1) * 512].rearrange("q (o t) -> q o t", o=OUT, t=4)
-                src = bc_view[:, g, :, :, n].rearrange("q t o -> q o t")
-                nc.vector.tensor_copy(out=dst, in_=src)
-        lwt = transpose_words(lw_raw[:].bitcast(F32))
-        copy_out(True, wg[:].bitcast(F32)[:, 5 * 512 : 6 * 512], lwt)
-        nc.vector.tensor_copy(out=pb[:], in_=pbb[:])
+        v_copies(0)
+        new_xg(1)
 
         for p in range(NCH + 2):
             due = list(range(p)) if p == WEIGHTS_AT + 1 else [p - 1] if p > WEIGHTS_AT + 1 else []
             sums = [p - 2] if p >= 2 else []
+            late = p == 2
             load(p + AHEAD)
             t_to_psum(p)
             tr(p + 2)
+            if p == 0:
+                lwt = transpose_words(lw_raw[:].bitcast(F32))
             for c in due:
                 if live(c):
                     mx(c)
             sq(p)
-            for c in sums:
-                s_epi(c)
+            if not late:
+                for c in sums:
+                    s_epi(c)
             s_tanh(p + 1)
             t4(p)
             g_round(p)
             s_copies(p + 2)
+            if late:
+                for c in sums:
+                    s_epi(c)
+            v_window(p)
+            if p == 0:
+                regroup(0)
+                v_copies(1)
+            v_copies(p + 2)
+            if not late:
+                for c in sums:
+                    v_epi(c)
+            v_work(p)
+            if late:
+                for c in sums:
+                    v_epi(c)
+            if p == 0:
+                regroup(1)
             if p == WEIGHTS_AT:
+                copy_out(True, wg[:].bitcast(F32)[:, 5 * 512 : 6 * 512], lwt)
+                nc.vector.tensor_copy(out=pb[:], in_=pbb[:])
                 quant(wc, wsp, 0, 1024, wg[:, 0:4096])
                 quant(wc, wsp, 1024, 1536, wg[:, 4096:6144])
-            v_window(p)
-            v_copies(p + 2)
-            for c in sums:
-                v_epi(c)
-            v_work(p)

@@ -21,9 +21,9 @@ FLOPS = 2 * ROWS * K * OUT * (POWERS + 1)
 SIZES = (1, 1, 2, 2, 2, 2, 2, 2, 2, 2, 2, 2, 2, 2, 2, 1, 1, 1, 1)
 NCH = len(SIZES)
 assert sum(SIZES) * P == ROWS
-V_COPIES = {c: (0,) for c in range(NCH) if c < 2 or (SIZES[c] == 2 and c % 2 == 0)}
-G_COLS = {c: 640 if c in V_COPIES else 416 for c in range(NCH)}
-G_CHUNKS = tuple(c for c in range(NCH) if SIZES[c] == 2)
+V_COPIES = {c: (0,) for c in range(NCH) if c < 2 or (SIZES[c] == 2 and c % 3 != 0)}
+G_COLS = {c: 768 if c + 2 in V_COPIES else 512 for c in range(NCH)}
+G_CHUNKS = tuple(range(2, 18))
 E_CHUNKS = G_CHUNKS
 V_SQUARES = ()
 S_ROUNDS = (18,)
@@ -210,9 +210,10 @@ def tile_kolmogorovarnoldlinear_t_kernel(tc, x, basis_coeffs, linear_w, pathway_
                 quant(cs[c], sps[c], 3 * w4, 5 * w4, b[:, w : 3 * w])
                 quant(cs[c], sps[c], w4, 2 * w4, b[:, 0:w])
             else:
-                quant(cs[c], sps[c], w4, 2 * w4, b[:, 0:w])
                 quant(cs[c], sps[c], 3 * w4, 5 * w4, b[:, w : 3 * w])
             quant(cs[c], sps[c], 2 * w4, 3 * w4, sb[:])
+            if c not in S_ROUNDS:
+                quant(cs[c], sps[c], w4, 2 * w4, b[:, 0:w])
 
         def mx_pass(dst, lw, ls, wi, g, start, stop):
             off = wi * 256 + g * P

@@ -21,8 +21,8 @@ FLOPS = 2 * ROWS * K * OUT * (POWERS + 1)
 SIZES = (1, 1, 2, 2, 2, 2, 2, 2, 2, 2, 2, 2, 2, 2, 2, 1, 1, 1, 1)
 NCH = len(SIZES)
 assert sum(SIZES) * P == ROWS
-V_COPIES = {c: (0,) for c in range(NCH) if c < 2 or (SIZES[c] == 2 and c % 3 != 0)}
-G_COLS = {c: 768 if c + 2 in V_COPIES else 512 for c in range(NCH)}
+V_COPIES = {c: (0,) for c in range(NCH) if c < 2 or (SIZES[c] == 2 and c > 2 and c % 4 != 2)}
+G_COLS = {c: 640 if c + 2 in V_COPIES else 448 for c in range(NCH)}
 G_CHUNKS = tuple(range(2, 18))
 E_CHUNKS = G_CHUNKS
 V_SQUARES = ()
@@ -151,12 +151,11 @@ def tile_kolmogorovarnoldlinear_t_kernel(tc, x, basis_coeffs, linear_w, pathway_
             if not live(c):
                 return
             w = SIZES[c] * K
-            bs[c] = bpool.tile([P, 3 * w], BF16, name="b", align_bytes=64)
-            square(c in V_FOURTHS, bs[c][:, 2 * w : 3 * w], fs[c][:, w : 2 * w])
+            bs[c] = bpool.tile([P, 2 * w], BF16, name="b", align_bytes=64)
+            square(c in V_FOURTHS, bs[c][:, w : 2 * w], fs[c][:, w : 2 * w])
+            sbs[c] = sqpool.tile([P, 2 * w], BF16, name="sb", align_bytes=64)
             if c in S_ROUNDS:
-                sbs[c] = sqpool.tile([P, w], BF16, name="sb", align_bytes=64)
-                nc.scalar.activation(out=bs[c][:, 0:w], in_=fs[c][:, 0:w], func=ACT.Copy)
-                nc.scalar.activation(out=sbs[c][:], in_=fs[c][:, w : 2 * w], func=ACT.Copy)
+                nc.scalar.activation(out=sbs[c][:], in_=fs[c][:], func=ACT.Copy)
 
         def t_to_psum(c):
             if not live(c) or c not in E_CHUNKS:
@@ -168,15 +167,13 @@ def tile_kolmogorovarnoldlinear_t_kernel(tc, x, basis_coeffs, linear_w, pathway_
                 ets[c].append(et)
 
         def g_round(c):
-            if not live(c) or c in S_ROUNDS:
+            if not live(c) or c not in G_CHUNKS:
                 return
-            w = SIZES[c] * K
-            sbs[c] = sqpool.tile([P, w], BF16, name="sb", align_bytes=64)
-            if c in G_CHUNKS:
-                n = SIZES[c] * G_COLS[c]
-                nc.gpsimd.tensor_scalar(
-                    out=sbs[c][:, 0:n], in0=fs[c][:, w : w + n], scalar1=1.0, scalar2=0.0, op0=ALU.mult, op1=ALU.add
-                )
+            hi = 2 * SIZES[c] * K
+            lo = hi - SIZES[c] * G_COLS[c]
+            nc.gpsimd.tensor_scalar(
+                out=sbs[c][:, lo:hi], in0=fs[c][:, lo:hi], scalar1=1.0, scalar2=0.0, op0=ALU.mult, op1=ALU.add
+            )
 
         def v_window(c):
             if not live(c) or c not in E_CHUNKS:
@@ -185,11 +182,19 @@ def tile_kolmogorovarnoldlinear_t_kernel(tc, x, basis_coeffs, linear_w, pathway_
             for j in range(SIZES[c]):
                 lo = j * 512
                 nc.vector.tensor_tensor(
-                    out=bs[c][:, w + lo : w + lo + 512], in0=fs[c][:, w + lo : w + lo + 512], in1=ets[c][j][:], op=ALU.mult
+                    out=bs[c][:, lo : lo + 512], in0=fs[c][:, w + lo : w + lo + 512], in1=ets[c][j][:], op=ALU.mult
                 )
 
         def quant(codes, planes, lo, hi, src):
             nc.vector.quantize_mx(out=codes[:, lo:hi].bitcast(FP8X4), scales=planes[:, lo:hi], in_=src)
+
+        def q_x(c):
+            if not live(c) or c in cs:
+                return
+            w4 = SIZES[c] * K // 4
+            cs[c] = cpool.tile([P, 5 * w4], U32, name="codes", align_bytes=64)
+            sps[c] = cpool.tile([P, 5 * w4], U8, name="planes", align_bytes=64)
+            quant(cs[c], sps[c], 0, w4, xgs[c][:])
 
         def v_work(c):
             if not live(c):
@@ -199,21 +204,15 @@ def tile_kolmogorovarnoldlinear_t_kernel(tc, x, basis_coeffs, linear_w, pathway_
             f, b, sb = fs[c], bs[c], sbs[c]
             done = 512 * SIZES[c] if c in E_CHUNKS else 0
             if c not in S_ROUNDS:
-                n = SIZES[c] * G_COLS[c] if c in G_CHUNKS else 0
-                nc.vector.tensor_copy(out=b[:, 0:w], in_=f[:, 0:w])
-                nc.vector.tensor_copy(out=sb[:, n:w], in_=f[:, w + n : 2 * w])
-            nc.vector.tensor_tensor(out=b[:, w + done : 2 * w], in0=f[:, w + done : 2 * w], in1=f[:, done:w], op=ALU.mult)
-            cs[c] = cpool.tile([P, 5 * w4], U32, name="codes", align_bytes=64)
-            sps[c] = cpool.tile([P, 5 * w4], U8, name="planes", align_bytes=64)
-            quant(cs[c], sps[c], 0, w4, xgs[c][:])
+                hi = 2 * w - (SIZES[c] * G_COLS[c] if c in G_CHUNKS else 0)
+                nc.vector.tensor_copy(out=sb[:, 0:hi], in_=f[:, 0:hi])
+            nc.vector.tensor_tensor(out=b[:, done:w], in0=f[:, w + done : 2 * w], in1=f[:, done:w], op=ALU.mult)
+            q_x(c)
             if c in S_ROUNDS:
-                quant(cs[c], sps[c], 3 * w4, 5 * w4, b[:, w : 3 * w])
-                quant(cs[c], sps[c], w4, 2 * w4, b[:, 0:w])
-            else:
-                quant(cs[c], sps[c], 3 * w4, 5 * w4, b[:, w : 3 * w])
-            quant(cs[c], sps[c], 2 * w4, 3 * w4, sb[:])
+                quant(cs[c], sps[c], 3 * w4, 5 * w4, b[:])
+            quant(cs[c], sps[c], w4, 3 * w4, sb[:])
             if c not in S_ROUNDS:
-                quant(cs[c], sps[c], w4, 2 * w4, b[:, 0:w])
+                quant(cs[c], sps[c], 3 * w4, 5 * w4, b[:])
 
         def mx_pass(dst, lw, ls, wi, g, start, stop):
             off = wi * 256 + g * P
@@ -276,8 +275,8 @@ def tile_kolmogorovarnoldlinear_t_kernel(tc, x, basis_coeffs, linear_w, pathway_
             )
 
         load(0)
-        load(1)
         load_coeffs(0)
+        load(1)
         load(2)
         load_coeffs(1)
         lw_raw = const.tile([P, K], BF16, name="lw_raw")
@@ -302,13 +301,13 @@ def tile_kolmogorovarnoldlinear_t_kernel(tc, x, basis_coeffs, linear_w, pathway_
         wg_view = wg[:, 0 : POWERS * K].rearrange("q (n g o t) -> q n g o t", n=POWERS, g=2, o=OUT, t=4)
 
         def regroup(g):
-            for n in range(POWERS):
-                nc.vector.tensor_copy(out=wg_view[:, n, g], in_=bc_view[:, g, :, :, n].rearrange("q t o -> q o t"))
+            nc.vector.tensor_copy(out=wg_view[:, :, g], in_=bc_view[:, g].rearrange("q t o n -> q n o t"))
 
         tr(0)
         tr(1)
         s_tanh(0)
         v_copies(0)
+        q_x(0)
         new_xg(1)
 
         for p in range(NCH + 2):
@@ -327,8 +326,12 @@ def tile_kolmogorovarnoldlinear_t_kernel(tc, x, basis_coeffs, linear_w, pathway_
             if not late:
                 for c in sums:
                     s_epi(c)
-            s_tanh(p + 1)
-            t4(p)
+            if p == 0:
+                t4(p)
+                s_tanh(p + 1)
+            else:
+                s_tanh(p + 1)
+                t4(p)
             g_round(p)
             s_copies(p + 2)
             if late:
@@ -337,8 +340,8 @@ def tile_kolmogorovarnoldlinear_t_kernel(tc, x, basis_coeffs, linear_w, pathway_
             v_window(p)
             if p == 0:
                 regroup(0)
-                v_copies(1)
-            v_copies(p + 2)
+            else:
+                v_copies(p + 2)
             if not late:
                 for c in sums:
                     v_epi(c)
@@ -347,6 +350,8 @@ def tile_kolmogorovarnoldlinear_t_kernel(tc, x, basis_coeffs, linear_w, pathway_
                 for c in sums:
                     v_epi(c)
             if p == 0:
+                v_copies(1)
+                v_copies(2)
                 regroup(1)
             if p == WEIGHTS_AT:
                 copy_out(True, wg[:].bitcast(F32)[:, 5 * 512 : 6 * 512], lwt)

@@ -21,10 +21,10 @@ FLOPS = 2 * ROWS * K * OUT * (POWERS + 1)
 SIZES = (1, 1, 2, 2, 2, 2, 2, 2, 2, 2, 2, 2, 2, 2, 2, 1, 1, 1, 1)
 NCH = len(SIZES)
 assert sum(SIZES) * P == ROWS
-V_COPIES = {c: (0,) for c in range(NCH) if c < 2 or (SIZES[c] == 2 and c > 2 and c % 4 != 2)}
-G_COLS = {c: 640 if c + 2 in V_COPIES else 448 for c in range(NCH)}
-G_CHUNKS = tuple(range(2, 18))
-E_CHUNKS = G_CHUNKS
+V_COPIES = {c: (0,) for c in range(NCH) if c < 2 or (SIZES[c] == 2 and c > 2 and c % 3 != 0)}
+E_PIECES = {c: 3 if SIZES[c] == 2 and c % 3 != 2 else SIZES[c] for c in range(2, 18)}
+G_UNIT = 480
+G_COLS = {c: G_UNIT * (E_PIECES[c] + len(V_COPIES.get(c + 2, ()))) for c in E_PIECES}
 V_SQUARES = ()
 S_ROUNDS = (18,)
 WEIGHTS_AT = 0
@@ -48,8 +48,7 @@ def tile_kolmogorovarnoldlinear_t_kernel(tc, x, basis_coeffs, linear_w, pathway_
         cpool = ctx.enter_context(tc.tile_pool(name="cpool", bufs=3))
         ypool = ctx.enter_context(tc.tile_pool(name="ypool", bufs=3))
         sqpool = ctx.enter_context(tc.tile_pool(name="sqpool", bufs=1))
-        tpsum = ctx.enter_context(tc.psum_pool(name="tpsum", bufs=4))
-        epsum = ctx.enter_context(tc.psum_pool(name="epsum", bufs=2))
+        tpsum = ctx.enter_context(tc.psum_pool(name="tpsum", bufs=6))
         apsum = ctx.enter_context(tc.psum_pool(name="apsum", bufs=2))
 
         xs = {}
@@ -158,31 +157,40 @@ def tile_kolmogorovarnoldlinear_t_kernel(tc, x, basis_coeffs, linear_w, pathway_
                 nc.scalar.activation(out=sbs[c][:], in_=fs[c][:], func=ACT.Copy)
 
         def t_to_psum(c):
-            if not live(c) or c not in E_CHUNKS:
+            if c not in E_PIECES:
                 return
             ets[c] = []
-            for j in range(SIZES[c]):
-                et = epsum.tile([P, 512], F32, name="et")
-                nc.tensor.matmul(out=et[:], lhsT=ident[:], rhs=fs[c][:, j * 512 : (j + 1) * 512], start=True, stop=True)
+            for j in range(E_PIECES[c]):
+                et = tpsum.tile([P, 4, P], F32, name="xt")
+                nc.tensor.matmul(
+                    out=et[:].rearrange("p b r -> p (b r)"),
+                    lhsT=ident[:],
+                    rhs=fs[c][:, j * 512 : (j + 1) * 512],
+                    start=True,
+                    stop=True,
+                )
                 ets[c].append(et)
 
         def g_round(c):
-            if not live(c) or c not in G_CHUNKS:
+            if c not in G_COLS:
                 return
             hi = 2 * SIZES[c] * K
-            lo = hi - SIZES[c] * G_COLS[c]
+            lo = hi - G_COLS[c]
             nc.gpsimd.tensor_scalar(
                 out=sbs[c][:, lo:hi], in0=fs[c][:, lo:hi], scalar1=1.0, scalar2=0.0, op0=ALU.mult, op1=ALU.add
             )
 
         def v_window(c):
-            if not live(c) or c not in E_CHUNKS:
+            if c not in E_PIECES:
                 return
             w = SIZES[c] * K
-            for j in range(SIZES[c]):
+            for j in range(E_PIECES[c]):
                 lo = j * 512
                 nc.vector.tensor_tensor(
-                    out=bs[c][:, lo : lo + 512], in0=fs[c][:, w + lo : w + lo + 512], in1=ets[c][j][:], op=ALU.mult
+                    out=bs[c][:, lo : lo + 512],
+                    in0=fs[c][:, w + lo : w + lo + 512],
+                    in1=ets[c][j][:].rearrange("p b r -> p (b r)"),
+                    op=ALU.mult,
                 )
 
         def quant(codes, planes, lo, hi, src):
@@ -202,9 +210,9 @@ def tile_kolmogorovarnoldlinear_t_kernel(tc, x, basis_coeffs, linear_w, pathway_
             w = SIZES[c] * K
             w4 = w // 4
             f, b, sb = fs[c], bs[c], sbs[c]
-            done = 512 * SIZES[c] if c in E_CHUNKS else 0
+            done = 512 * E_PIECES.get(c, 0)
             if c not in S_ROUNDS:
-                hi = 2 * w - (SIZES[c] * G_COLS[c] if c in G_CHUNKS else 0)
+                hi = 2 * w - G_COLS.get(c, 0)
                 nc.vector.tensor_copy(out=sb[:, 0:hi], in_=f[:, 0:hi])
             nc.vector.tensor_tensor(out=b[:, done:w], in0=f[:, w + done : 2 * w], in1=f[:, done:w], op=ALU.mult)
             q_x(c)
@@ -301,7 +309,10 @@ def tile_kolmogorovarnoldlinear_t_kernel(tc, x, basis_coeffs, linear_w, pathway_
         wg_view = wg[:, 0 : POWERS * K].rearrange("q (n g o t) -> q n g o t", n=POWERS, g=2, o=OUT, t=4)
 
         def regroup(g):
-            nc.vector.tensor_copy(out=wg_view[:, :, g], in_=bc_view[:, g].rearrange("q t o n -> q n o t"))
+            nc.vector.tensor_copy(
+                out=wg_view[:, :, g].rearrange("q n (h o) t -> q h n o t", h=2),
+                in_=bc_view[:, g].rearrange("q t (h o) n -> q h n o t", h=2),
+            )
 
         tr(0)
         tr(1)

@@ -18,15 +18,15 @@ OUT = 128
 POWERS = 5
 FLOPS = 2 * ROWS * K * OUT * (POWERS + 1)
 
-SIZES = (1, 1, 2, 2, 2, 2, 2, 2, 2, 2, 2, 2, 2, 2, 2, 1, 1, 1, 1)
+SIZES = (1,) + (2,) * 14 + (1,) * 3
 NCH = len(SIZES)
 assert sum(SIZES) * P == ROWS
-V_COPIES = {c: (0,) for c in range(NCH) if c < 2 or (SIZES[c] == 2 and c > 2 and c % 3 != 0)}
-E_PIECES = {c: 3 if SIZES[c] == 2 and c % 3 != 2 else SIZES[c] for c in range(2, 18)}
+V_COPIES = {0: (0,), 1: (0, 1), **{c: (0,) for c in range(3, NCH) if SIZES[c] == 2 and c % 3 != 0}}
+E_PIECES = {c: 3 if SIZES[c] == 2 and c % 3 != 0 else SIZES[c] for c in range(2, NCH - 1)}
 G_UNIT = 480
 G_COLS = {c: G_UNIT * (E_PIECES[c] + len(V_COPIES.get(c + 2, ()))) for c in E_PIECES}
 V_SQUARES = ()
-S_ROUNDS = (18,)
+S_ROUNDS = (NCH - 1,)
 WEIGHTS_AT = 0
 V_FOURTHS = ()
 AHEAD = 5
@@ -131,12 +131,14 @@ def tile_kolmogorovarnoldlinear_t_kernel(tc, x, basis_coeffs, linear_w, pathway_
             w = SIZES[c] * K
             fs[c] = fpool.tile([P, 2 * w], F32, name="f")
             if c in PSUM_TANH:
-                for g in range(2):
-                    nc.scalar.activation(
-                        out=fs[c][:, g * 512 : (g + 1) * 512].rearrange("p (r u e) -> p r u e", r=P, u=2, e=2),
-                        in_=xts[c][0][:, 2 * g : 2 * g + 2, :].bitcast(BF16).rearrange("p u (r e) -> p r u e", r=P, e=2),
-                        func=ACT.Tanh,
-                    )
+                for j in range(SIZES[c]):
+                    for g in range(2):
+                        lo = j * K + g * 512
+                        nc.scalar.activation(
+                            out=fs[c][:, lo : lo + 512].rearrange("p (r u e) -> p r u e", r=P, u=2, e=2),
+                            in_=xts[c][j][:, 2 * g : 2 * g + 2, :].bitcast(BF16).rearrange("p u (r e) -> p r u e", r=P, e=2),
+                            func=ACT.Tanh,
+                        )
             else:
                 nc.scalar.activation(out=fs[c][:, 0:w], in_=xgs[c][:], func=ACT.Tanh)
 

@@ -21,15 +21,16 @@ FLOPS = 2 * ROWS * K * OUT * (POWERS + 1)
 SIZES = (1,) + (2,) * 14 + (1,) * 3
 NCH = len(SIZES)
 assert sum(SIZES) * P == ROWS
-V_COPIES = {0: (0,), 1: (0, 1), **{c: (0,) for c in range(3, NCH) if SIZES[c] == 2 and c % 3 != 0}}
+V_COPIES = {0: (0,), 1: (0, 1), **{c: (0,) for c in range(3, NCH) if SIZES[c] == 2 and c % 5 != 2}}
 E_PIECES = {c: 3 if SIZES[c] == 2 and c % 3 != 0 else SIZES[c] for c in range(2, NCH - 1)}
-G_UNIT = 480
+G_UNIT = 496
 G_COLS = {c: G_UNIT * (E_PIECES[c] + len(V_COPIES.get(c + 2, ()))) for c in E_PIECES}
 V_SQUARES = ()
 S_ROUNDS = (NCH - 1,)
 WEIGHTS_AT = 0
 V_FOURTHS = ()
 AHEAD = 5
+GP = 3
 PSUM_TANH = (0, 1)
 
 
@@ -84,9 +85,10 @@ def tile_kolmogorovarnoldlinear_t_kernel(tc, x, basis_coeffs, linear_w, pathway_
                 nc.tensor.transpose(xt[:, b, :], src_words[:, b * P : (b + 1) * P], ident[:])
             return xt
 
-        def copy_out(on_vector, dst_words, xt):
-            dst = dst_words.rearrange("p (g r u) -> p g r u", g=2, r=P, u=2)
-            src = xt[:].rearrange("p (g u) r -> p g r u", g=2, u=2)
+        def copy_out(on_vector, dst_words, xt, halves=(0, 1)):
+            n, lo = len(halves), halves[0]
+            dst = dst_words[:, lo * 256 : (lo + n) * 256].rearrange("p (g r u) -> p g r u", g=n, r=P, u=2)
+            src = xt[:, 2 * lo : 2 * (lo + n), :].rearrange("p (g u) r -> p g r u", g=n, u=2)
             if on_vector:
                 nc.vector.tensor_copy(out=dst, in_=src)
             else:
@@ -96,17 +98,29 @@ def tile_kolmogorovarnoldlinear_t_kernel(tc, x, basis_coeffs, linear_w, pathway_
             if not live(c):
                 return
             words = xs[c][:].bitcast(F32)
-            xts[c] = [transpose_words(words[:, j, :]) for j in range(SIZES[c])]
+            if c == 0:
+                xts[c] = []
+                for g in range(2):
+                    xt = tpsum.tile([P, 4, P], F32, name="xt")
+                    for b in (2 * g, 2 * g + 1):
+                        nc.tensor.transpose(xt[:, b, :], words[:, 0, b * P : (b + 1) * P], ident[:])
+                    xts[c].append(xt)
+            else:
+                xts[c] = [transpose_words(words[:, j, :]) for j in range(SIZES[c])]
 
         def new_xg(c):
             if c not in xgs:
                 xgs[c] = gpool.tile([P, SIZES[c] * K], BF16, name="xg", align_bytes=64)
 
-        def v_copies(c):
+        def v_copies(c, halves=(0, 1)):
             if not live(c):
                 return
             new_xg(c)
             words = xgs[c][:].bitcast(F32)
+            if c == 0:
+                for g in halves:
+                    copy_out(True, words, xts[c][g], halves=(g,))
+                return
             for j in V_COPIES.get(c, ()):
                 copy_out(True, words[:, j * 512 : (j + 1) * 512], xts[c][j])
 
@@ -125,18 +139,19 @@ def tile_kolmogorovarnoldlinear_t_kernel(tc, x, basis_coeffs, linear_w, pathway_
             else:
                 nc.scalar.activation(out=dst, in_=src, func=ACT.Square)
 
-        def s_tanh(c):
+        def s_tanh(c, halves=None):
             if not live(c):
                 return
             w = SIZES[c] * K
-            fs[c] = fpool.tile([P, 2 * w], F32, name="f")
+            if c not in fs:
+                fs[c] = fpool.tile([P, 2 * w], F32, name="f")
             if c in PSUM_TANH:
                 for j in range(SIZES[c]):
-                    for g in range(2):
+                    for g in range(2) if halves is None else halves:
                         lo = j * K + g * 512
                         nc.scalar.activation(
                             out=fs[c][:, lo : lo + 512].rearrange("p (r u e) -> p r u e", r=P, u=2, e=2),
-                            in_=xts[c][j][:, 2 * g : 2 * g + 2, :].bitcast(BF16).rearrange("p u (r e) -> p r u e", r=P, e=2),
+                            in_=xts[c][g if c == 0 else j][:, 2 * g : 2 * g + 2, :].bitcast(BF16).rearrange("p u (r e) -> p r u e", r=P, e=2),
                             func=ACT.Tanh,
                         )
             else:
@@ -310,16 +325,30 @@ def tile_kolmogorovarnoldlinear_t_kernel(tc, x, basis_coeffs, linear_w, pathway_
         bc_view = bc_raw[:].rearrange("q (g t o n) -> q g t o n", g=2, t=4, o=OUT, n=POWERS)
         wg_view = wg[:, 0 : POWERS * K].rearrange("q (n g o t) -> q n g o t", n=POWERS, g=2, o=OUT, t=4)
 
-        def regroup(g):
+        one = const.tile([P, 1], F32, name="one")
+
+        def regroup(g, powers):
             nc.vector.tensor_copy(
-                out=wg_view[:, :, g].rearrange("q n (h o) t -> q h n o t", h=2),
-                in_=bc_view[:, g].rearrange("q t (h o) n -> q h n o t", h=2),
+                out=wg_view[:, 0:powers, g].rearrange("q n (h o) t -> q h n o t", h=2),
+                in_=bc_view[:, g, :, :, 0:powers].rearrange("q t (h o) n -> q h n o t", h=2),
+            )
+
+        def g_regroup(g, powers):
+            nc.gpsimd.tensor_scalar(
+                out=wg_view[:, powers:POWERS, g],
+                in0=bc_view[:, g, :, :, powers:POWERS].rearrange("q t o n -> q n o t"),
+                scalar1=one[:, 0:1],
+                scalar2=0.0,
+                op0=ALU.mult,
+                op1=ALU.add,
             )
 
         tr(0)
         tr(1)
-        s_tanh(0)
-        v_copies(0)
+        s_tanh(0, halves=(0,))
+        v_copies(0, halves=(1,))
+        s_tanh(0, halves=(1,))
+        v_copies(0, halves=(0,))
         q_x(0)
         new_xg(1)
 
@@ -352,7 +381,7 @@ def tile_kolmogorovarnoldlinear_t_kernel(tc, x, basis_coeffs, linear_w, pathway_
                     s_epi(c)
             v_window(p)
             if p == 0:
-                regroup(0)
+                regroup(0, POWERS)
             else:
                 v_copies(p + 2)
             if not late:
@@ -363,11 +392,12 @@ def tile_kolmogorovarnoldlinear_t_kernel(tc, x, basis_coeffs, linear_w, pathway_
                 for c in sums:
                     v_epi(c)
             if p == 0:
+                nc.vector.memset(one[:], 1.0)
+                g_regroup(1, GP)
                 v_copies(1)
-                v_copies(2)
-                regroup(1)
-            if p == WEIGHTS_AT:
                 copy_out(True, wg[:].bitcast(F32)[:, 5 * 512 : 6 * 512], lwt)
+                regroup(1, GP)
+            if p == WEIGHTS_AT:
                 nc.vector.tensor_copy(out=pb[:], in_=pbb[:])
                 quant(wc, wsp, 0, 1024, wg[:, 0:4096])
                 quant(wc, wsp, 1024, 1536, wg[:, 4096:6144])

@@ -21,9 +21,9 @@ FLOPS = 2 * ROWS * K * OUT * (POWERS + 1)
 SIZES = (1,) + (2,) * 14 + (1,) * 3
 NCH = len(SIZES)
 assert sum(SIZES) * P == ROWS
-V_COPIES = {0: (0,), 1: (0, 1), **{c: (0,) for c in range(3, NCH) if SIZES[c] == 2 and c % 5 != 2}}
+V_COPIES = {0: (0,), 1: (0, 1), **{c: (0,) for c in range(4, NCH) if SIZES[c] == 2}}
 E_PIECES = {c: 3 if SIZES[c] == 2 and c % 3 != 0 else SIZES[c] for c in range(2, NCH - 1)}
-G_UNIT = 496
+G_UNIT = 528
 G_COLS = {c: G_UNIT * (E_PIECES[c] + len(V_COPIES.get(c + 2, ()))) for c in E_PIECES}
 V_SQUARES = ()
 S_ROUNDS = (NCH - 1,)

@@ -23,7 +23,7 @@ NCH = len(SIZES)
 assert sum(SIZES) * P == ROWS
 V_COPIES = {0: (0,), 1: (0, 1), **{c: (0,) for c in range(4, NCH) if SIZES[c] == 2}}
 E_PIECES = {c: 3 if SIZES[c] == 2 and c % 3 != 0 else SIZES[c] for c in range(2, NCH - 1)}
-G_UNIT = 528
+G_UNIT = 576
 G_COLS = {c: G_UNIT * (E_PIECES[c] + len(V_COPIES.get(c + 2, ()))) for c in E_PIECES}
 V_SQUARES = ()
 S_ROUNDS = (NCH - 1,)
@@ -398,6 +398,6 @@ def tile_kolmogorovarnoldlinear_t_kernel(tc, x, basis_coeffs, linear_w, pathway_
                 copy_out(True, wg[:].bitcast(F32)[:, 5 * 512 : 6 * 512], lwt)
                 regroup(1, GP)
             if p == WEIGHTS_AT:
-                nc.vector.tensor_copy(out=pb[:], in_=pbb[:])
+                nc.gpsimd.tensor_copy(out=pb[:], in_=pbb[:])
                 quant(wc, wsp, 0, 1024, wg[:, 0:4096])
                 quant(wc, wsp, 1024, 1536, wg[:, 4096:6144])

from contextlib import ExitStack

import concourse.mybir as mybir
from concourse.masks import make_identity

FP8X4 = mybir.dt.float8_e4m3fn_x4
BF16 = mybir.dt.bfloat16
F32 = mybir.dt.float32
U32 = mybir.dt.uint32
U8 = mybir.dt.uint8
ACT = mybir.ActivationFunctionType
ALU = mybir.AluOpType

P = 128
ROWS = 4096
K = 1024
OUT = 128
POWERS = 5
FLOPS = 2 * ROWS * K * OUT * (POWERS + 1)

SIZES = (1,) + (2,) * 14 + (1,) * 3
NCH = len(SIZES)
assert sum(SIZES) * P == ROWS
V_COPIES = {0: (0,), 1: (0, 1), **{c: (0,) for c in range(4, NCH) if SIZES[c] == 2}}
E_PIECES = {c: 3 if SIZES[c] == 2 and c % 3 != 0 else SIZES[c] for c in range(2, NCH - 1)}
G_UNIT = 576
G_COLS = {c: G_UNIT * (E_PIECES[c] + len(V_COPIES.get(c + 2, ()))) for c in E_PIECES}
V_SQUARES = ()
S_ROUNDS = (NCH - 1,)
WEIGHTS_AT = 0
V_FOURTHS = ()
AHEAD = 5
GP = 3
PSUM_TANH = (0, 1)


def tile_kolmogorovarnoldlinear_t_kernel(tc, x, basis_coeffs, linear_w, pathway_balance, out):
    nc = tc.nc
    xf = x.flatten_outer_dims()
    of = out.flatten_outer_dims()
    row0 = [P * sum(SIZES[:c]) for c in range(NCH)]
    with ExitStack() as ctx:
        ctx.enter_context(tc.manual_schedule())
        const = ctx.enter_context(tc.tile_pool(name="const", bufs=1))
        xpool = ctx.enter_context(tc.tile_pool(name="xpool", bufs=6))
        gpool = ctx.enter_context(tc.tile_pool(name="gpool", bufs=3))
        fpool = ctx.enter_context(tc.tile_pool(name="fpool", bufs=3))
        bpool = ctx.enter_context(tc.tile_pool(name="bpool", bufs=3))
        cpool = ctx.enter_context(tc.tile_pool(name="cpool", bufs=3))
        ypool = ctx.enter_context(tc.tile_pool(name="ypool", bufs=3))
        sqpool = ctx.enter_context(tc.tile_pool(name="sqpool", bufs=1))
        tpsum = ctx.enter_context(tc.psum_pool(name="tpsum", bufs=6))
        apsum = ctx.enter_context(tc.psum_pool(name="apsum", bufs=2))

        xs = {}
        xts = {}
        xgs = {}
        fs = {}
        bs = {}
        cs = {}
        sps = {}
        sbs = {}
        ets = {}
        accn = {}
        accl = {}
        tmps = {}

        def live(c):
            return 0 <= c < NCH

        def load(c):
            if not live(c):
                return
            r = SIZES[c]
            xs[c] = xpool.tile([P, r, K], BF16, name="xs")
            src = xf[row0[c] : row0[c] + P * r, :].rearrange("(p j) k -> p j k", j=r)
            parts = 2 if c == 0 else 1
            for i in range(parts):
                cols = slice(i * K // parts, (i + 1) * K // parts)
                nc.sync.dma_start(out=xs[c][:, :, cols], in_=src[:, :, cols])

        def transpose_words(src_words):
            xt = tpsum.tile([P, 4, P], F32, name="xt")
            for b in range(4):
                nc.tensor.transpose(xt[:, b, :], src_words[:, b * P : (b + 1) * P], ident[:])
            return xt

        def copy_out(on_vector, dst_words, xt, halves=(0, 1)):
            n, lo = len(halves), halves[0]
            dst = dst_words[:, lo * 256 : (lo + n) * 256].rearrange("p (g r u) -> p g r u", g=n, r=P, u=2)
            src = xt[:, 2 * lo : 2 * (lo + n), :].rearrange("p (g u) r -> p g r u", g=n, u=2)
            if on_vector:
                nc.vector.tensor_copy(out=dst, in_=src)
            else:
                nc.scalar.copy(out=dst, in_=src)

        def tr(c):
            if not live(c):
                return
            words = xs[c][:].bitcast(F32)
            if c == 0:
                xts[c] = []
                for g in range(2):
                    xt = tpsum.tile([P, 4, P], F32, name="xt")
                    for b in (2 * g, 2 * g + 1):
                        nc.tensor.transpose(xt[:, b, :], words[:, 0, b * P : (b + 1) * P], ident[:])
                    xts[c].append(xt)
            else:
                xts[c] = [transpose_words(words[:, j, :]) for j in range(SIZES[c])]

        def new_xg(c):
            if c not in xgs:
                xgs[c] = gpool.tile([P, SIZES[c] * K], BF16, name="xg", align_bytes=64)

        def v_copies(c, halves=(0, 1)):
            if not live(c):
                return
            new_xg(c)
            words = xgs[c][:].bitcast(F32)
            if c == 0:
                for g in halves:
                    copy_out(True, words, xts[c][g], halves=(g,))
                return
            for j in V_COPIES.get(c, ()):
                copy_out(True, words[:, j * 512 : (j + 1) * 512], xts[c][j])

        def s_copies(c):
            if not live(c):
                return
            new_xg(c)
            words = xgs[c][:].bitcast(F32)
            for j in range(SIZES[c]):
                if j not in V_COPIES.get(c, ()):
                    copy_out(False, words[:, j * 512 : (j + 1) * 512], xts[c][j])

        def square(on_vector, dst, src):
            if on_vector:
                nc.vector.tensor_tensor(out=dst, in0=src, in1=src, op=ALU.mult)
            else:
                nc.scalar.activation(out=dst, in_=src, func=ACT.Square)

        def s_tanh(c, halves=None):
            if not live(c):
                return
            w = SIZES[c] * K
            if c not in fs:
                fs[c] = fpool.tile([P, 2 * w], F32, name="f")
            if c in PSUM_TANH:
                for j in range(SIZES[c]):
                    for g in range(2) if halves is None else halves:
                        lo = j * K + g * 512
                        nc.scalar.activation(
                            out=fs[c][:, lo : lo + 512].rearrange("p (r u e) -> p r u e", r=P, u=2, e=2),
                            in_=xts[c][g if c == 0 else j][:, 2 * g : 2 * g + 2, :].bitcast(BF16).rearrange("p u (r e) -> p r u e", r=P, e=2),
                            func=ACT.Tanh,
                        )
            else:
                nc.scalar.activation(out=fs[c][:, 0:w], in_=xgs[c][:], func=ACT.Tanh)

        def sq(c):
            if not live(c):
                return
            w = SIZES[c] * K
            square(c in V_SQUARES, fs[c][:, w : 2 * w], fs[c][:, 0:w])

        def t4(c):
            if not live(c):
                return
            w = SIZES[c] * K
            bs[c] = bpool.tile([P, 2 * w], BF16, name="b", align_bytes=64)
            square(c in V_FOURTHS, bs[c][:, w : 2 * w], fs[c][:, w : 2 * w])
            sbs[c] = sqpool.tile([P, 2 * w], BF16, name="sb", align_bytes=64)
            if c in S_ROUNDS:
                nc.scalar.activation(out=sbs[c][:], in_=fs[c][:], func=ACT.Copy)

        def t_to_psum(c):
            if c not in E_PIECES:
                return
            ets[c] = []
            for j in range(E_PIECES[c]):
                et = tpsum.tile([P, 4, P], F32, name="xt")
                nc.tensor.matmul(
                    out=et[:].rearrange("p b r -> p (b r)"),
                    lhsT=ident[:],
                    rhs=fs[c][:, j * 512 : (j + 1) * 512],
                    start=True,
                    stop=True,
                )
                ets[c].append(et)

        def g_round(c):
            if c not in G_COLS:
                return
            hi = 2 * SIZES[c] * K
            lo = hi - G_COLS[c]
            nc.gpsimd.tensor_scalar(
                out=sbs[c][:, lo:hi], in0=fs[c][:, lo:hi], scalar1=1.0, scalar2=0.0, op0=ALU.mult, op1=ALU.add
            )

        def v_window(c):
            if c not in E_PIECES:
                return
            w = SIZES[c] * K
            for j in range(E_PIECES[c]):
                lo = j * 512
                nc.vector.tensor_tensor(
                    out=bs[c][:, lo : lo + 512],
                    in0=fs[c][:, w + lo : w + lo + 512],
                    in1=ets[c][j][:].rearrange("p b r -> p (b r)"),
                    op=ALU.mult,
                )

        def quant(codes, planes, lo, hi, src):
            nc.vector.quantize_mx(out=codes[:, lo:hi].bitcast(FP8X4), scales=planes[:, lo:hi], in_=src)

        def q_x(c):
            if not live(c) or c in cs:
                return
            w4 = SIZES[c] * K // 4
            cs[c] = cpool.tile([P, 5 * w4], U32, name="codes", align_bytes=64)
            sps[c] = cpool.tile([P, 5 * w4], U8, name="planes", align_bytes=64)
            quant(cs[c], sps[c], 0, w4, xgs[c][:])

        def v_work(c):
            if not live(c):
                return
            w = SIZES[c] * K
            w4 = w // 4
            f, b, sb = fs[c], bs[c], sbs[c]
            done = 512 * E_PIECES.get(c, 0)
            if c not in S_ROUNDS:
                hi = 2 * w - G_COLS.get(c, 0)
                nc.vector.tensor_copy(out=sb[:, 0:hi], in_=f[:, 0:hi])
            nc.vector.tensor_tensor(out=b[:, done:w], in0=f[:, w + done : 2 * w], in1=f[:, done:w], op=ALU.mult)
            q_x(c)
            if c in S_ROUNDS:
                quant(cs[c], sps[c], 3 * w4, 5 * w4, b[:])
            quant(cs[c], sps[c], w4, 3 * w4, sb[:])
            if c not in S_ROUNDS:
                quant(cs[c], sps[c], 3 * w4, 5 * w4, b[:])

        def mx_pass(dst, lw, ls, wi, g, start, stop):
            off = wi * 256 + g * P
            nc.tensor.matmul_mx(
                out=dst,
                lhsT=lw.bitcast(FP8X4),
                lhsT_scale=ls,
                rhs=wc[:, off : off + P].bitcast(FP8X4),
                rhs_scale=wsp[:, off : off + P],
                start=start,
                stop=stop,
            )

        def mx(c):
            if not live(c):
                return
            w4 = SIZES[c] * K // 4
            acc = apsum.tile([P, 2, SIZES[c], OUT], F32, name="acc")
            accl[c], accn[c] = acc[:, 0], acc[:, 1]
            for j in range(SIZES[c]):
                for g in range(2):
                    off = (j * 2 + g) * P
                    mx_pass(accl[c][:, j, :], cs[c][:, off : off + P], sps[c][:, off : off + P], POWERS, g, g == 0, g == 1)
            order = (0, 3, 4, 1, 2) if c in S_ROUNDS else (0, 1, 2, 3, 4)
            for j in range(SIZES[c]):
                for n in order:
                    for g in range(2):
                        if n == 0:
                            lw, ls = onec[:], onesp[:]
                        else:
                            off = n * w4 + (j * 2 + g) * P
                            lw, ls = cs[c][:, off : off + P], sps[c][:, off : off + P]
                        mx_pass(accn[c][:, j, :], lw, ls, n, g, n == order[0] and g == 0, n == order[-1] and g == 1)

        def s_epi(c):
            if not live(c):
                return
            tmps[c] = ypool.tile([P, SIZES[c], OUT], F32, name="tmp")
            nc.scalar.activation(out=tmps[c][:], in_=accl[c], func=ACT.Copy, scale=pb[:, 1:2])

        def v_epi(c):
            if not live(c):
                return
            r = SIZES[c]
            y = ypool.tile([P, r, OUT], F32, name="y")
            nc.vector.scalar_tensor_tensor(
                out=y[:], in0=accn[c], scalar=pb[:, 0:1], in1=tmps[c][:], op0=ALU.mult, op1=ALU.add
            )
            nc.sync.dma_start(
                out=of[row0[c] : row0[c] + P * r, :].rearrange("(p j) o -> p j o", j=r), in_=y[:]
            )

        half = 2 * 2 * OUT * POWERS
        bc_raw = const.tile([P, 2 * half], BF16, name="bc_raw")

        def load_coeffs(g):
            nc.sync.dma_start(
                out=bc_raw[:, g * half : (g + 1) * half].rearrange("q (u e f) -> q u e f", u=2, e=2),
                in_=basis_coeffs[g * 512 : (g + 1) * 512].rearrange("(u q e) o n -> q u e (o n)", u=2, q=P, e=2),
            )

        load(0)
        load_coeffs(0)
        load(1)
        load(2)
        load_coeffs(1)
        lw_raw = const.tile([P, K], BF16, name="lw_raw")
        nc.sync.dma_start(out=lw_raw[:], in_=linear_w)
        pbb = const.tile([P, 2], BF16, name="pbb")
        nc.sync.dma_start(out=pbb[:], in_=pathway_balance.partition_broadcast(P))
        for c in range(3, AHEAD):
            load(c)

        ident = const.tile([P, P], F32, name="ident")
        make_identity(nc, ident[:])
        ones_b = const.tile([P, 4 * P], BF16, name="ones_b", align_bytes=64)
        nc.vector.memset(ones_b[:], 1.0)
        onec = const.tile([P, P], U32, name="onec", align_bytes=64)
        onesp = const.tile([P, P], U8, name="onesp", align_bytes=64)
        nc.vector.quantize_mx(out=onec[:].bitcast(FP8X4), scales=onesp[:], in_=ones_b[:])
        wg = const.tile([P, 6 * K], BF16, name="wg", align_bytes=64)
        wc = const.tile([P, 6 * 256], U32, name="wc", align_bytes=64)
        wsp = const.tile([P, 6 * 256], U8, name="wsp", align_bytes=64)
        pb = const.tile([P, 2], F32, name="pb")
        bc_view = bc_raw[:].rearrange("q (g t o n) -> q g t o n", g=2, t=4, o=OUT, n=POWERS)
        wg_view = wg[:, 0 : POWERS * K].rearrange("q (n g o t) -> q n g o t", n=POWERS, g=2, o=OUT, t=4)

        one = const.tile([P, 1], F32, name="one")

        def regroup(g, powers):
            nc.vector.tensor_copy(
                out=wg_view[:, 0:powers, g].rearrange("q n (h o) t -> q h n o t", h=2),
                in_=bc_view[:, g, :, :, 0:powers].rearrange("q t (h o) n -> q h n o t", h=2),
            )

        def g_regroup(g, powers):
            nc.gpsimd.tensor_scalar(
                out=wg_view[:, powers:POWERS, g],
                in0=bc_view[:, g, :, :, powers:POWERS].rearrange("q t o n -> q n o t"),
                scalar1=one[:, 0:1],
                scalar2=0.0,
                op0=ALU.mult,
                op1=ALU.add,
            )

        tr(0)
        tr(1)
        s_tanh(0, halves=(0,))
        v_copies(0, halves=(1,))
        s_tanh(0, halves=(1,))
        v_copies(0, halves=(0,))
        q_x(0)
        new_xg(1)

        for p in range(NCH + 2):
            due = list(range(p)) if p == WEIGHTS_AT + 1 else [p - 1] if p > WEIGHTS_AT + 1 else []
            sums = [p - 2] if p >= 2 else []
            late = p == 2
            load(p + AHEAD)
            t_to_psum(p)
            tr(p + 2)
            if p == 0:
                lwt = transpose_words(lw_raw[:].bitcast(F32))
            for c in due:
                if live(c):
                    mx(c)
            sq(p)
            if not late:
                for c in sums:
                    s_epi(c)
            if p == 0:
                t4(p)
                s_tanh(p + 1)
            else:
                s_tanh(p + 1)
                t4(p)
            g_round(p)
            s_copies(p + 2)
            if late:
                for c in sums:
                    s_epi(c)
            v_window(p)
            if p == 0:
                regroup(0, POWERS)
            else:
                v_copies(p + 2)
            if not late:
                for c in sums:
                    v_epi(c)
            v_work(p)
            if late:
                for c in sums:
                    v_epi(c)
            if p == 0:
                nc.vector.memset(one[:], 1.0)
                g_regroup(1, GP)
                v_copies(1)
                copy_out(True, wg[:].bitcast(F32)[:, 5 * 512 : 6 * 512], lwt)
                regroup(1, GP)
            if p == WEIGHTS_AT:
                nc.gpsimd.tensor_copy(out=pb[:], in_=pbb[:])
                quant(wc, wsp, 0, 1024, wg[:, 0:4096])
                quant(wc, wsp, 1024, 1536, wg[:, 4096:6144])
